import numpy as np
import ml_dtypes


def mxq(x, axis, fmt="e4m3"):
    dtype, down = {"e4m3": (ml_dtypes.float8_e4m3fn, 7), "e5m2": (ml_dtypes.float8_e5m2, 14)}[fmt]
    v = np.moveaxis(np.asarray(x, np.float32).astype(ml_dtypes.bfloat16).astype(np.float64), axis, -1)
    blocks = v.reshape(v.shape[:-1] + (-1, 32))
    amax = np.abs(blocks).max(-1, keepdims=True)
    byte = np.maximum(np.where(amax > 0, np.frexp(amax)[1] - 1 + 127, 0) - down, 1)
    scale = np.exp2(byte - 127.0)
    codes = (blocks / scale).astype(np.float32).astype(dtype).astype(np.float64)
    return np.moveaxis((codes * scale).reshape(v.shape), -1, axis)


WIDE = False


def mx_kscale(k):
    if not WIDE:
        return np.ones(k)
    levels = np.array([10, -10, 5, -5, 0])
    a = np.random.permutation(np.resize(levels, k // 512 * 4)).reshape(k // 512, 4)
    idx = np.arange(k)
    return np.exp2(a[idx // 512, idx % 128 // 32])


BF16 = ml_dtypes.bfloat16


def bf(x):
    return np.asarray(x, np.float32).astype(BF16)


def f64(x):
    return np.asarray(x).astype(np.float64)


N, F, U, G, P = 4096, 512, 256, 3, 3
C = G + P
T = G + 2 * P + 1
LO, HI = -1.0, 1.0
LN_EPS = 0.001


def b_splines(x, grid):
    xe = x[..., None]
    bases = np.where((xe >= grid[..., :-1]) & (xe < grid[..., 1:]), 1.0, 0.0)
    for k in range(1, P + 1):
        left = (xe - grid[..., :-(k + 1)]) / (grid[..., k:-1] - grid[..., :-(k + 1)])
        right = (grid[..., k + 1:] - xe) / (grid[..., k + 1:] - grid[..., 1:-k])
        bases = left * bases[..., :-1] + right * bases[..., 1:]
    return bases.reshape(x.shape[0], -1)


def setup_inputs():
    t = mx_kscale(F)
    h = (HI - LO) / G
    knots = np.linspace(LO - P * h, LO + (G + P) * h, T)
    grid = knots[None, None, :] + (np.random.random_sample((1, F, T)) - 0.5) * 0.25 * h
    return {
        "x": bf(np.random.standard_normal((N, F)) * 0.1 + np.random.standard_normal((N, 1)) * 0.1),
        "ln_gamma": bf((1.0 + 0.1 * np.random.standard_normal(F)) * t),
        "ln_beta": bf(0.1 * np.random.standard_normal(F) * t),
        "base_weight": bf(np.random.standard_normal((F, U)) / np.sqrt(F) / t[:, None]),
        "base_bias": bf(0.25 * np.random.standard_normal(U)),
        "spline_weight": bf(np.random.standard_normal((F * C, U)) / np.sqrt(F)),
        "grid": bf(grid * t[None, :, None]),
    }


def reference(x, ln_gamma, ln_beta, base_weight, base_bias, spline_weight, grid):
    x = f64(x)
    mean = x.mean(-1, keepdims=True)
    var = x.var(-1, keepdims=True)
    xn = (x - mean) / np.sqrt(var + LN_EPS) * f64(ln_gamma) + f64(ln_beta)
    base_out = (mxq(np.maximum(xn, 0.0), 1, "e4m3") @ mxq(f64(base_weight), 0, "e4m3")) + f64(base_bias)
    spline_out = mxq(b_splines(xn, f64(grid)), 1, "e4m3") @ mxq(f64(spline_weight), 0, "e4m3")
    return base_out + spline_out

@@ -1,0 +1,230 @@
+from contextlib import ExitStack
+
+import concourse.mybir as mybir
+from concourse.masks import make_identity
+
+F32 = mybir.dt.float32
+BF16 = mybir.dt.bfloat16
+U32 = mybir.dt.uint32
+U8 = mybir.dt.uint8
+FP8X4 = mybir.dt.float8_e4m3fn_x4
+ALU = mybir.AluOpType
+ACT = mybir.ActivationFunctionType
+
+P = 128
+PACK = 4
+ROWS = 4096
+FEATURES = 512
+UNITS = 256
+KNOTS = 10
+BASES = 6
+CHUNKS = FEATURES // P
+PLANES = CHUNKS * BASES
+SPLINE_PASSES = PLANES // PACK
+PASSES = 1 + SPLINE_PASSES
+BLOCK = 512
+ROW_TILES = BLOCK // P
+BLOCKS = ROWS // BLOCK
+LN_EPS = 0.001
+
+FLOPS = 2 * ROWS * (FEATURES + FEATURES * BASES) * UNITS
+
+
+def tile_kanlinear_pa_t_kernel(
+    tc, x, ln_gamma, ln_beta, base_weight, base_bias, spline_weight, grid, out
+):
+    nc = tc.nc
+    with ExitStack() as ctx:
+        const = ctx.enter_context(tc.tile_pool(name="const", bufs=1))
+        wprep = ctx.enter_context(tc.tile_pool(name="wprep", bufs=1))
+        rows_pool = ctx.enter_context(tc.tile_pool(name="rows", bufs=2))
+        small = ctx.enter_context(tc.tile_pool(name="small", bufs=2))
+        xn_pool = ctx.enter_context(tc.tile_pool(name="xn", bufs=2))
+        work = ctx.enter_context(tc.tile_pool(name="work", bufs=4))
+        planes = ctx.enter_context(tc.tile_pool(name="planes", bufs=3))
+        mx = ctx.enter_context(tc.tile_pool(name="mx", bufs=2))
+        psum_t = ctx.enter_context(tc.psum_pool(name="psum_t", bufs=4))
+        psum_o = ctx.enter_context(tc.psum_pool(name="psum_o", bufs=2))
+
+        ident = const.tile([P, P], F32)
+        make_identity(nc, ident[:])
+
+        knots_bf = const.tile([P, CHUNKS, KNOTS], BF16)
+        nc.sync.dma_start(out=knots_bf[:], in_=grid.rearrange("o (c p) t -> p (o c) t", p=P))
+        gamma_bf = const.tile([P, CHUNKS], BF16)
+        beta_bf = const.tile([P, CHUNKS], BF16)
+        with nc.allow_non_contiguous_dma(reason="512 elements, one per partition and chunk"):
+            nc.sync.dma_start(out=gamma_bf[:], in_=ln_gamma.rearrange("(c p) -> p c", p=P))
+            nc.sync.dma_start(out=beta_bf[:], in_=ln_beta.rearrange("(c p) -> p c", p=P))
+        bias_bf = const.tile([P, UNITS], BF16)
+        nc.sync.dma_start(out=bias_bf[:], in_=base_bias.partition_broadcast(P))
+
+        gamma = const.tile([P, CHUNKS], F32)
+        beta = const.tile([P, CHUNKS], F32)
+        bias = const.tile([P, UNITS], F32)
+        knots = const.tile([P, CHUNKS, KNOTS], F32)
+        nc.vector.tensor_copy(out=gamma[:], in_=gamma_bf[:])
+        nc.vector.tensor_copy(out=beta[:], in_=beta_bf[:])
+        nc.vector.tensor_copy(out=bias[:], in_=bias_bf[:])
+        nc.vector.tensor_copy(out=knots[:], in_=knots_bf[:])
+        neg_knots = const.tile([P, CHUNKS, KNOTS], F32)
+        nc.vector.tensor_scalar_mul(out=neg_knots[:], in0=knots[:], scalar1=-1.0)
+        neg_half = const.tile([P, ROW_TILES], F32)
+        nc.vector.memset(neg_half[:], -0.5)
+
+        span = {}
+        for s in (1, 2, 3, 4):
+            span[s] = const.tile([P, CHUNKS, KNOTS - s], F32, name="span%d" % s)
+            nc.vector.tensor_sub(out=span[s][:], in0=knots[:, :, s:KNOTS], in1=knots[:, :, 0 : KNOTS - s])
+        inv_span1 = const.tile([P, CHUNKS, KNOTS - 1], F32)
+        nc.vector.reciprocal(out=inv_span1[:], in_=span[1][:])
+
+        ENDS = KNOTS - 3
+        rise = const.tile([P, CHUNKS, ENDS], F32)
+        neg_fall = const.tile([P, CHUNKS, ENDS], F32)
+        prod = const.tile([P, CHUNKS, ENDS], F32)
+        nc.vector.tensor_mul(out=prod[:], in0=span[1][:, :, 0:ENDS], in1=span[2][:, :, 0:ENDS])
+        nc.vector.tensor_mul(out=prod[:], in0=prod[:], in1=span[3][:])
+        nc.vector.reciprocal(out=rise[:], in_=prod[:])
+        prod2 = const.tile([P, CHUNKS, ENDS], F32)
+        nc.vector.tensor_mul(out=prod2[:], in0=span[1][:, :, 2 : 2 + ENDS], in1=span[2][:, :, 1 : 1 + ENDS])
+        nc.vector.tensor_mul(out=prod2[:], in0=prod2[:], in1=span[3][:])
+        nc.vector.reciprocal(out=neg_fall[:], in_=prod2[:])
+        nc.vector.tensor_scalar_mul(out=neg_fall[:], in0=neg_fall[:], scalar1=-1.0)
+        neg_lam = const.tile([P, CHUNKS, BASES], F32)
+        neg_mu = const.tile([P, CHUNKS, BASES], F32)
+        nc.vector.tensor_mul(out=neg_lam[:], in0=span[4][:], in1=inv_span1[:, :, 0:BASES])
+        nc.vector.tensor_scalar_mul(out=neg_lam[:], in0=neg_lam[:], scalar1=-1.0)
+        nc.vector.tensor_mul(out=neg_mu[:], in0=span[4][:], in1=inv_span1[:, :, 3 : 3 + BASES])
+        nc.vector.tensor_scalar_mul(out=neg_mu[:], in0=neg_mu[:], scalar1=-1.0)
+
+        w_raw = wprep.tile([P, PASSES * PACK, UNITS], BF16)
+        nc.scalar.dma_start(out=w_raw[:, 0:PACK, :], in_=base_weight.rearrange("(t p) u -> p t u", p=P))
+        nc.scalar.dma_start(
+            out=w_raw[:, PACK:, :].rearrange("p (c j) u -> p c (j u)", j=BASES),
+            in_=spline_weight.rearrange("(c p j) u -> p c (j u)", p=P, j=BASES),
+        )
+        w_grouped = wprep.tile([P, PASSES, UNITS, PACK], BF16, align_bytes=64)
+        w_codes = const.tile([P, PASSES, UNITS], U32, align_bytes=64)
+        w_scales = const.tile([P, PASSES, UNITS], U8, align_bytes=64)
+        for c in range(PASSES):
+            nc.vector.tensor_copy(
+                out=w_grouped[:, c, :, :],
+                in_=w_raw[:, c * PACK : (c + 1) * PACK, :].rearrange("p t u -> p u t"),
+            )
+        for c in range(PASSES):
+            nc.vector.quantize_mx(
+                out=w_codes[:, c, :].bitcast(FP8X4),
+                scales=w_scales[:, c, :],
+                in_=w_grouped[:, c, :, :].rearrange("p u t -> p (u t)"),
+            )
+
+        x_blocks = x.rearrange("(b t p) f -> b p t f", t=ROW_TILES, p=P)
+        out_blocks = out.rearrange("(b t p) u -> b p t u", t=ROW_TILES, p=P)
+
+        for b in range(BLOCKS):
+            x_sb = rows_pool.tile([P, ROW_TILES, FEATURES], BF16)
+            nc.sync.dma_start(out=x_sb[:], in_=x_blocks[b])
+            stats = small.tile([P, ROW_TILES, 6], F32)
+            mean_var = small.tile([P, ROW_TILES, 2], F32)
+            for t in range(ROW_TILES):
+                nc.vector.bn_stats(out=stats[:, t, :], in_=x_sb[:, t, :])
+                nc.vector.bn_aggr(out=mean_var[:, t, :], in_=stats[:, t, :])
+            var_eps = small.tile([P, ROW_TILES], F32)
+            nc.vector.tensor_scalar_add(out=var_eps[:], in0=mean_var[:, :, 1], scalar1=LN_EPS)
+            rstd = small.tile([P, ROW_TILES], F32)
+            nc.gpsimd.tensor_tensor(out=rstd[:], in0=var_eps[:], in1=neg_half[:], op=ALU.pow)
+            z = rows_pool.tile([P, ROW_TILES, FEATURES], F32)
+            for t in range(ROW_TILES):
+                nc.vector.tensor_scalar(
+                    out=z[:, t, :], in0=x_sb[:, t, :],
+                    scalar1=mean_var[:, t, 0:1], scalar2=rstd[:, t : t + 1],
+                    op0=ALU.subtract, op1=ALU.mult,
+                )
+
+            xn = xn_pool.tile([P, CHUNKS, BLOCK], F32)
+            for c in range(CHUNKS):
+                z_t = psum_t.tile([P, BLOCK], F32)
+                for t in range(ROW_TILES):
+                    nc.tensor.transpose(z_t[:, t * P : (t + 1) * P], z[:, t, c * P : (c + 1) * P], ident[:])
+                nc.scalar.activation(
+                    out=xn[:, c, :], in_=z_t[:], func=ACT.Identity,
+                    scale=gamma[:, c : c + 1], bias=beta[:, c : c + 1],
+                )
+
+            codes = mx.tile([P, PASSES, BLOCK], U32, align_bytes=64)
+            scales = mx.tile([P, PASSES, BLOCK], U8, align_bytes=64)
+
+            relu_grouped = planes.tile([P, BLOCK, PACK], BF16, align_bytes=64, tag="grouped")
+            nc.scalar.activation(out=relu_grouped[:], in_=xn[:].rearrange("p t n -> p n t"), func=ACT.Relu)
+            nc.vector.quantize_mx(
+                out=codes[:, 0, :].bitcast(FP8X4), scales=scales[:, 0, :],
+                in_=relu_grouped[:].rearrange("p n t -> p (n t)"),
+            )
+
+            left = {}
+            right = {}
+            for c in range(CHUNKS):
+                v = xn[:, c, :]
+                up = {}
+                down = {}
+                for i in range(KNOTS):
+                    square = work.tile([P, BLOCK], F32, tag="square")
+                    nc.scalar.activation(out=square[:], in_=v, func=ACT.Square, bias=neg_knots[:, c, i : i + 1])
+                    cube = work.tile([P, BLOCK], F32, tag="cube")
+                    nc.vector.scalar_tensor_tensor(
+                        out=cube[:], in0=v, scalar=knots[:, c, i : i + 1], in1=square[:],
+                        op0=ALU.subtract, op1=ALU.mult,
+                    )
+                    if i <= 6:
+                        up[i] = work.tile([P, BLOCK], F32, name="up", tag="up")
+                        nc.scalar.activation(out=up[i][:], in_=cube[:], func=ACT.Relu, scale=rise[:, c, i : i + 1])
+                    if i >= 3:
+                        down[i] = work.tile([P, BLOCK], F32, name="down", tag="down")
+                        nc.scalar.activation(
+                            out=down[i][:], in_=cube[:], func=ACT.Relu, scale=neg_fall[:, c, i - 3 : i - 2]
+                        )
+                    if 1 <= i <= 6:
+                        j = i - 1
+                        group, slot = divmod(c * BASES + j, PACK)
+                        if slot == 0:
+                            left[group] = planes.tile([P, PACK, BLOCK], BF16, name="left", tag="left")
+                        nc.vector.scalar_tensor_tensor(
+                            out=left[group][:, slot, :], in0=up[i][:], scalar=neg_lam[:, c, j : j + 1],
+                            in1=up[i - 1][:], op0=ALU.mult, op1=ALU.add,
+                        )
+                    if i >= 4:
+                        j = i - 4
+                        group, slot = divmod(c * BASES + j, PACK)
+                        if slot == 0:
+                            right[group] = planes.tile([P, PACK, BLOCK], BF16, name="right", tag="right")
+                        nc.vector.scalar_tensor_tensor(
+                            out=right[group][:, slot, :], in0=down[i - 1][:], scalar=neg_mu[:, c, j : j + 1],
+                            in1=down[i][:], op0=ALU.mult, op1=ALU.add,
+                        )
+                        if slot == PACK - 1:
+                            grouped = planes.tile([P, BLOCK, PACK], BF16, align_bytes=64, tag="grouped")
+                            nc.vector.tensor_tensor(
+                                out=grouped[:],
+                                in0=left[group][:].rearrange("p t n -> p n t"),
+                                in1=right[group][:].rearrange("p t n -> p n t"),
+                                op=ALU.max,
+                            )
+                            nc.vector.quantize_mx(
+                                out=codes[:, 1 + group, :].bitcast(FP8X4), scales=scales[:, 1 + group, :],
+                                in_=grouped[:].rearrange("p n t -> p (n t)"),
+                            )
+
+            result = rows_pool.tile([P, ROW_TILES, UNITS], F32)
+            for t in range(ROW_TILES):
+                cols = slice(t * P, (t + 1) * P)
+                acc = psum_o.tile([P, UNITS], F32)
+                for k in range(PASSES):
+                    nc.tensor.matmul_mx(
+                        out=acc[:],
+                        lhsT=codes[:, k, cols].bitcast(FP8X4), lhsT_scale=scales[:, k, cols],
+                        rhs=w_codes[:, k, :].bitcast(FP8X4), rhs_scale=w_scales[:, k, :],
+                        start=(k == 0), stop=(k == PASSES - 1),
+                    )
+                nc.vector.tensor_add(out=result[:, t, :], in0=acc[:], in1=bias[:])
+            nc.sync.dma_start(out=out_blocks[b], in_=result[:])

@@ -22,9 +22,11 @@ CHUNKS = FEATURES // P
 PLANES = CHUNKS * BASES
 SPLINE_PASSES = PLANES // PACK
 PASSES = 1 + SPLINE_PASSES
-BLOCK = 512
-ROW_TILES = BLOCK // P
+BLOCK = 1024
 BLOCKS = ROWS // BLOCK
+BANK = 512
+ROW_TILES = BANK // P
+BANKS = BLOCK // BANK
 LN_EPS = 0.001
 
 FLOPS = 2 * ROWS * (FEATURES + FEATURES * BASES) * UNITS
@@ -36,28 +38,29 @@ def tile_kanlinear_pa_t_kernel(
     nc = tc.nc
     with ExitStack() as ctx:
         const = ctx.enter_context(tc.tile_pool(name="const", bufs=1))
-        wprep = ctx.enter_context(tc.tile_pool(name="wprep", bufs=1))
+        wprep = ctx.enter_context(tc.tile_pool(name="wprep", bufs=2))
         rows_pool = ctx.enter_context(tc.tile_pool(name="rows", bufs=2))
         small = ctx.enter_context(tc.tile_pool(name="small", bufs=2))
         xn_pool = ctx.enter_context(tc.tile_pool(name="xn", bufs=2))
-        work = ctx.enter_context(tc.tile_pool(name="work", bufs=4))
-        planes = ctx.enter_context(tc.tile_pool(name="planes", bufs=3))
-        mx = ctx.enter_context(tc.tile_pool(name="mx", bufs=2))
+        work = ctx.enter_context(tc.tile_pool(name="work", bufs=3))
+        halves = ctx.enter_context(tc.tile_pool(name="halves", bufs=4))
+        planes = ctx.enter_context(tc.tile_pool(name="planes", bufs=2))
+        mx = ctx.enter_context(tc.tile_pool(name="mx", bufs=1))
         psum_t = ctx.enter_context(tc.psum_pool(name="psum_t", bufs=4))
-        psum_o = ctx.enter_context(tc.psum_pool(name="psum_o", bufs=2))
+        psum_o = ctx.enter_context(tc.psum_pool(name="psum_o", bufs=4))
 
         ident = const.tile([P, P], F32)
         make_identity(nc, ident[:])
 
         knots_bf = const.tile([P, CHUNKS, KNOTS], BF16)
-        nc.sync.dma_start(out=knots_bf[:], in_=grid.rearrange("o (c p) t -> p (o c) t", p=P))
+        nc.scalar.dma_start(out=knots_bf[:], in_=grid.rearrange("o (c p) t -> p (o c) t", p=P))
         gamma_bf = const.tile([P, CHUNKS], BF16)
         beta_bf = const.tile([P, CHUNKS], BF16)
         with nc.allow_non_contiguous_dma(reason="512 elements, one per partition and chunk"):
-            nc.sync.dma_start(out=gamma_bf[:], in_=ln_gamma.rearrange("(c p) -> p c", p=P))
-            nc.sync.dma_start(out=beta_bf[:], in_=ln_beta.rearrange("(c p) -> p c", p=P))
+            nc.scalar.dma_start(out=gamma_bf[:], in_=ln_gamma.rearrange("(c p) -> p c", p=P))
+            nc.scalar.dma_start(out=beta_bf[:], in_=ln_beta.rearrange("(c p) -> p c", p=P))
         bias_bf = const.tile([P, UNITS], BF16)
-        nc.sync.dma_start(out=bias_bf[:], in_=base_bias.partition_broadcast(P))
+        nc.scalar.dma_start(out=bias_bf[:], in_=base_bias.partition_broadcast(P))
 
         gamma = const.tile([P, CHUNKS], F32)
         beta = const.tile([P, CHUNKS], F32)
@@ -98,133 +101,232 @@ def tile_kanlinear_pa_t_kernel(
         nc.vector.tensor_mul(out=neg_mu[:], in0=span[4][:], in1=inv_span1[:, :, 3 : 3 + BASES])
         nc.vector.tensor_scalar_mul(out=neg_mu[:], in0=neg_mu[:], scalar1=-1.0)
 
-        w_raw = wprep.tile([P, PASSES * PACK, UNITS], BF16)
+
+        w_raw = wprep.tile([P, PASSES * PACK, UNITS], BF16, bufs=1)
         nc.scalar.dma_start(out=w_raw[:, 0:PACK, :], in_=base_weight.rearrange("(t p) u -> p t u", p=P))
         nc.scalar.dma_start(
             out=w_raw[:, PACK:, :].rearrange("p (c j) u -> p c (j u)", j=BASES),
             in_=spline_weight.rearrange("(c p j) u -> p c (j u)", p=P, j=BASES),
         )
-        w_grouped = wprep.tile([P, PASSES, UNITS, PACK], BF16, align_bytes=64)
         w_codes = const.tile([P, PASSES, UNITS], U32, align_bytes=64)
         w_scales = const.tile([P, PASSES, UNITS], U8, align_bytes=64)
-        for c in range(PASSES):
-            nc.vector.tensor_copy(
-                out=w_grouped[:, c, :, :],
-                in_=w_raw[:, c * PACK : (c + 1) * PACK, :].rearrange("p t u -> p u t"),
-            )
-        for c in range(PASSES):
-            nc.vector.quantize_mx(
-                out=w_codes[:, c, :].bitcast(FP8X4),
-                scales=w_scales[:, c, :],
-                in_=w_grouped[:, c, :, :].rearrange("p u t -> p (u t)"),
-            )
 
-        x_blocks = x.rearrange("(b t p) f -> b p t f", t=ROW_TILES, p=P)
-        out_blocks = out.rearrange("(b t p) u -> b p t u", t=ROW_TILES, p=P)
+        def quantise_weights():
+            for k in range(PASSES):
+                w_grouped = wprep.tile([P, UNITS, PACK], BF16, align_bytes=64)
+                nc.vector.tensor_copy(
+                    out=w_grouped[:], in_=w_raw[:, k * PACK : (k + 1) * PACK, :].rearrange("p t u -> p u t")
+                )
+                nc.vector.quantize_mx(
+                    out=w_codes[:, k, :].bitcast(FP8X4),
+                    scales=w_scales[:, k, :],
+                    in_=w_grouped[:].rearrange("p u t -> p (u t)"),
+                )
 
-        for b in range(BLOCKS):
-            x_sb = rows_pool.tile([P, ROW_TILES, FEATURES], BF16)
-            nc.sync.dma_start(out=x_sb[:], in_=x_blocks[b])
+        x_banks = x.rearrange("(b t p) f -> b p t f", t=ROW_TILES, p=P)
+        out_banks = out.rearrange("(b t p) u -> b p t u", t=ROW_TILES, p=P)
+
+        x_sb, row_scale, row_shift, z_t, xn = {}, {}, {}, {}, {}
+        square, cube, up, down = {}, {}, {}, {}
+        left, right, grouped, codes, scales, acc = {}, {}, {}, {}, {}, {}
+
+        def load_rows(bank):
+            x_sb[bank] = rows_pool.tile([P, ROW_TILES, FEATURES], BF16, name="x_sb")
+            nc.sync.dma_start(out=x_sb[bank][:], in_=x_banks[bank])
+
+        def row_statistics(bank):
             stats = small.tile([P, ROW_TILES, 6], F32)
             mean_var = small.tile([P, ROW_TILES, 2], F32)
             for t in range(ROW_TILES):
-                nc.vector.bn_stats(out=stats[:, t, :], in_=x_sb[:, t, :])
+                nc.vector.bn_stats(out=stats[:, t, :], in_=x_sb[bank][:, t, :])
                 nc.vector.bn_aggr(out=mean_var[:, t, :], in_=stats[:, t, :])
             var_eps = small.tile([P, ROW_TILES], F32)
             nc.vector.tensor_scalar_add(out=var_eps[:], in0=mean_var[:, :, 1], scalar1=LN_EPS)
-            rstd = small.tile([P, ROW_TILES], F32)
-            nc.gpsimd.tensor_tensor(out=rstd[:], in0=var_eps[:], in1=neg_half[:], op=ALU.pow)
-            z = rows_pool.tile([P, ROW_TILES, FEATURES], F32)
-            for t in range(ROW_TILES):
-                nc.vector.tensor_scalar(
-                    out=z[:, t, :], in0=x_sb[:, t, :],
-                    scalar1=mean_var[:, t, 0:1], scalar2=rstd[:, t : t + 1],
-                    op0=ALU.subtract, op1=ALU.mult,
-                )
+            neg_mean = small.tile([P, ROW_TILES], F32)
+            nc.vector.tensor_scalar_mul(out=neg_mean[:], in0=mean_var[:, :, 0], scalar1=-1.0)
+            row_scale[bank] = small.tile([P, ROW_TILES], F32, name="row_scale")
+            nc.gpsimd.tensor_tensor(out=row_scale[bank][:], in0=var_eps[:], in1=neg_half[:], op=ALU.pow)
+            row_shift[bank] = small.tile([P, ROW_TILES], F32, name="row_shift")
+            nc.gpsimd.tensor_tensor(out=row_shift[bank][:], in0=neg_mean[:], in1=row_scale[bank][:], op=ALU.mult)
 
-            xn = xn_pool.tile([P, CHUNKS, BLOCK], F32)
-            for c in range(CHUNKS):
-                z_t = psum_t.tile([P, BLOCK], F32)
-                for t in range(ROW_TILES):
-                    nc.tensor.transpose(z_t[:, t * P : (t + 1) * P], z[:, t, c * P : (c + 1) * P], ident[:])
+        def normalise_and_transpose(bank):
+            z = rows_pool.tile([P, ROW_TILES, FEATURES], F32, bufs=1)
+            for t in range(ROW_TILES):
                 nc.scalar.activation(
-                    out=xn[:, c, :], in_=z_t[:], func=ACT.Identity,
+                    out=z[:, t, :], in_=x_sb[bank][:, t, :], func=ACT.Identity,
+                    scale=row_scale[bank][:, t : t + 1], bias=row_shift[bank][:, t : t + 1],
+                )
+            for c in range(CHUNKS):
+                z_t[bank, c] = psum_t.tile([P, BANK], F32, name="z_t")
+                for t in range(ROW_TILES):
+                    nc.tensor.transpose(
+                        z_t[bank, c][:, t * P : (t + 1) * P], z[:, t, c * P : (c + 1) * P], ident[:]
+                    )
+
+        def gamma_beta(bank):
+            b, h = divmod(bank, BANKS)
+            if h == 0:
+                xn[b] = xn_pool.tile([P, CHUNKS, BLOCK], F32, name="xn")
+            for c in range(CHUNKS):
+                nc.scalar.activation(
+                    out=xn[b][:, c, h * BANK : (h + 1) * BANK], in_=z_t[bank, c][:], func=ACT.Identity,
                     scale=gamma[:, c : c + 1], bias=beta[:, c : c + 1],
                 )
 
-            codes = mx.tile([P, PASSES, BLOCK], U32, align_bytes=64)
-            scales = mx.tile([P, PASSES, BLOCK], U8, align_bytes=64)
+        def relu_branch(b):
+            grouped[b, "relu"] = planes.tile([P, BLOCK, PACK], BF16, align_bytes=64, name="grouped")
+            nc.scalar.activation(out=grouped[b, "relu"][:], in_=xn[b][:].rearrange("p t n -> p n t"), func=ACT.Relu)
 
-            relu_grouped = planes.tile([P, BLOCK, PACK], BF16, align_bytes=64, tag="grouped")
-            nc.scalar.activation(out=relu_grouped[:], in_=xn[:].rearrange("p t n -> p n t"), func=ACT.Relu)
+        def quantise(b, key, k):
+            if b not in codes:
+                codes[b] = mx.tile([P, PASSES, BLOCK], U32, align_bytes=64, name="codes")
+                scales[b] = mx.tile([P, PASSES, BLOCK], U8, align_bytes=64, name="scales")
             nc.vector.quantize_mx(
-                out=codes[:, 0, :].bitcast(FP8X4), scales=scales[:, 0, :],
-                in_=relu_grouped[:].rearrange("p n t -> p (n t)"),
+                out=codes[b][:, k, :].bitcast(FP8X4), scales=scales[b][:, k, :],
+                in_=grouped[b, key][:].rearrange("p n t -> p (n t)"),
             )
 
-            left = {}
-            right = {}
-            for c in range(CHUNKS):
-                v = xn[:, c, :]
-                up = {}
-                down = {}
-                for i in range(KNOTS):
-                    square = work.tile([P, BLOCK], F32, tag="square")
-                    nc.scalar.activation(out=square[:], in_=v, func=ACT.Square, bias=neg_knots[:, c, i : i + 1])
-                    cube = work.tile([P, BLOCK], F32, tag="cube")
-                    nc.vector.scalar_tensor_tensor(
-                        out=cube[:], in0=v, scalar=knots[:, c, i : i + 1], in1=square[:],
-                        op0=ALU.subtract, op1=ALU.mult,
-                    )
-                    if i <= 6:
-                        up[i] = work.tile([P, BLOCK], F32, name="up", tag="up")
-                        nc.scalar.activation(out=up[i][:], in_=cube[:], func=ACT.Relu, scale=rise[:, c, i : i + 1])
-                    if i >= 3:
-                        down[i] = work.tile([P, BLOCK], F32, name="down", tag="down")
-                        nc.scalar.activation(
-                            out=down[i][:], in_=cube[:], func=ACT.Relu, scale=neg_fall[:, c, i - 3 : i - 2]
-                        )
-                    if 1 <= i <= 6:
-                        j = i - 1
-                        group, slot = divmod(c * BASES + j, PACK)
-                        if slot == 0:
-                            left[group] = planes.tile([P, PACK, BLOCK], BF16, name="left", tag="left")
-                        nc.vector.scalar_tensor_tensor(
-                            out=left[group][:, slot, :], in0=up[i][:], scalar=neg_lam[:, c, j : j + 1],
-                            in1=up[i - 1][:], op0=ALU.mult, op1=ALU.add,
-                        )
-                    if i >= 4:
-                        j = i - 4
-                        group, slot = divmod(c * BASES + j, PACK)
-                        if slot == 0:
-                            right[group] = planes.tile([P, PACK, BLOCK], BF16, name="right", tag="right")
-                        nc.vector.scalar_tensor_tensor(
-                            out=right[group][:, slot, :], in0=down[i - 1][:], scalar=neg_mu[:, c, j : j + 1],
-                            in1=down[i][:], op0=ALU.mult, op1=ALU.add,
-                        )
-                        if slot == PACK - 1:
-                            grouped = planes.tile([P, BLOCK, PACK], BF16, align_bytes=64, tag="grouped")
-                            nc.vector.tensor_tensor(
-                                out=grouped[:],
-                                in0=left[group][:].rearrange("p t n -> p n t"),
-                                in1=right[group][:].rearrange("p t n -> p n t"),
-                                op=ALU.max,
-                            )
-                            nc.vector.quantize_mx(
-                                out=codes[:, 1 + group, :].bitcast(FP8X4), scales=scales[:, 1 + group, :],
-                                in_=grouped[:].rearrange("p n t -> p (n t)"),
-                            )
+        steps = [(b, c, i) for b in range(BLOCKS) for c in range(CHUNKS) for i in range(KNOTS)]
 
-            result = rows_pool.tile([P, ROW_TILES, UNITS], F32)
+        def square_of(s):
+            b, c, i = steps[s]
+            square[s] = work.tile([P, BLOCK], F32, name="square")
+            nc.scalar.activation(
+                out=square[s][:], in_=xn[b][:, c, :], func=ACT.Square, bias=neg_knots[:, c, i : i + 1]
+            )
+
+        def cube_of(s):
+            b, c, i = steps[s]
+            cube[s] = work.tile([P, BLOCK], F32, name="cube")
+            nc.vector.scalar_tensor_tensor(
+                out=cube[s][:], in0=xn[b][:, c, :], scalar=knots[:, c, i : i + 1], in1=square[s][:],
+                op0=ALU.subtract, op1=ALU.mult,
+            )
+
+        def halves_of(s):
+            b, c, i = steps[s]
+            if i <= 6:
+                up[s] = halves.tile([P, BLOCK], F32, name="up")
+                nc.scalar.activation(out=up[s][:], in_=cube[s][:], func=ACT.Relu, scale=rise[:, c, i : i + 1])
+            if i >= 3:
+                down[s] = halves.tile([P, BLOCK], F32, name="down")
+                nc.scalar.activation(
+                    out=down[s][:], in_=cube[s][:], func=ACT.Relu, scale=neg_fall[:, c, i - 3 : i - 2]
+                )
+
+        def group_done_at(s):
+            b, c, i = steps[s]
+            if i < 4:
+                return None
+            group, slot = divmod(c * BASES + i - 4, PACK)
+            return group if slot == PACK - 1 else None
+
+        def forms_of(s):
+            b, c, i = steps[s]
+            if 1 <= i <= 6:
+                j = i - 1
+                group, slot = divmod(c * BASES + j, PACK)
+                if slot == 0:
+                    left[b, group] = planes.tile([P, PACK, BLOCK], BF16, name="left")
+                nc.vector.scalar_tensor_tensor(
+                    out=left[b, group][:, slot, :], in0=up[s][:], scalar=neg_lam[:, c, j : j + 1],
+                    in1=up[s - 1][:], op0=ALU.mult, op1=ALU.add,
+                )
+            if i >= 4:
+                j = i - 4
+                group, slot = divmod(c * BASES + j, PACK)
+                if slot == 0:
+                    right[b, group] = planes.tile([P, PACK, BLOCK], BF16, name="right")
+                nc.vector.scalar_tensor_tensor(
+                    out=right[b, group][:, slot, :], in0=down[s - 1][:], scalar=neg_mu[:, c, j : j + 1],
+                    in1=down[s][:], op0=ALU.mult, op1=ALU.add,
+                )
+            group = group_done_at(s)
+            if group is not None:
+                nc.vector.tensor_tensor(
+                    out=left[b, group][:].rearrange("p t n -> p (t n)"),
+                    in0=left[b, group][:].rearrange("p t n -> p (t n)"),
+                    in1=right[b, group][:].rearrange("p t n -> p (t n)"),
+                    op=ALU.max,
+                )
+
+        def regroup_at(s):
+            b = steps[s][0]
+            group = group_done_at(s)
+            if group is not None:
+                grouped[b, group] = planes.tile([P, BLOCK, PACK], BF16, align_bytes=64, name="grouped")
+                dst = grouped[b, group][:].rearrange("p (a i) t -> p a t i", i=4)
+                src = left[b, group][:].rearrange("p t (a i) -> p a t i", i=4)
+                if group % 2 == 0:
+                    nc.vector.tensor_copy(out=dst, in_=src)
+                else:
+                    nc.scalar.copy(out=dst, in_=src)
+
+        def quantise_at(s):
+            group = group_done_at(s)
+            if group is not None:
+                quantise(steps[s][0], group, 1 + group)
+
+        def multiply(bank):
+            b, h = divmod(bank, BANKS)
             for t in range(ROW_TILES):
-                cols = slice(t * P, (t + 1) * P)
-                acc = psum_o.tile([P, UNITS], F32)
+                cols = slice((h * ROW_TILES + t) * P, (h * ROW_TILES + t + 1) * P)
+                acc[bank, t] = psum_o.tile([P, UNITS], F32, name="acc")
                 for k in range(PASSES):
                     nc.tensor.matmul_mx(
-                        out=acc[:],
-                        lhsT=codes[:, k, cols].bitcast(FP8X4), lhsT_scale=scales[:, k, cols],
+                        out=acc[bank, t][:],
+                        lhsT=codes[b][:, k, cols].bitcast(FP8X4), lhsT_scale=scales[b][:, k, cols],
                         rhs=w_codes[:, k, :].bitcast(FP8X4), rhs_scale=w_scales[:, k, :],
                         start=(k == 0), stop=(k == PASSES - 1),
                     )
-                nc.vector.tensor_add(out=result[:, t, :], in0=acc[:], in1=bias[:])
-            nc.sync.dma_start(out=out_blocks[b], in_=result[:])
+
+        def add_bias_and_store(bank):
+            result = rows_pool.tile([P, ROW_TILES, UNITS], F32)
+            for t in range(ROW_TILES):
+                nc.vector.tensor_add(out=result[:, t, :], in0=acc[bank, t][:], in1=bias[:])
+            nc.sync.dma_start(out=out_banks[bank], in_=result[:])
+
+        def side_jobs(s):
+            b, c, i = steps[s]
+            if c < BANKS and b + 1 < BLOCKS:
+                bank = (b + 1) * BANKS + c
+                if i == 0:
+                    load_rows(bank)
+                if i == 3:
+                    row_statistics(bank)
+                if i == 5:
+                    normalise_and_transpose(bank)
+                if i == 7:
+                    gamma_beta(bank)
+            if c == 2 and i == 0:
+                relu_branch(b)
+            if c == 2 and i == 2:
+                quantise(b, "relu", 0)
+
+        def products_after(s):
+            b, c, i = steps[s]
+            return b if (c == CHUNKS - 1 and i == KNOTS - 1) else None
+
+        for bank in range(BANKS):
+            load_rows(bank)
+        for bank in range(BANKS):
+            row_statistics(bank)
+        quantise_weights()
+        for bank in range(BANKS):
+            normalise_and_transpose(bank)
+            gamma_beta(bank)
+
+        stages = (square_of, cube_of, halves_of, forms_of, regroup_at, quantise_at)
+        for r in range(len(steps) + len(stages) + BANKS):
+            if r < len(steps):
+                side_jobs(r)
+            for lag, stage in enumerate(stages):
+                if 0 <= r - lag < len(steps):
+                    stage(r - lag)
+            for h in range(BANKS):
+                s = r - len(stages) - h
+                if 0 <= s < len(steps) and products_after(s) is not None:
+                    multiply(products_after(s) * BANKS + h)
+                s = s - 1
+                if 0 <= s < len(steps) and products_after(s) is not None:
+                    add_bias_and_store(products_after(s) * BANKS + h)

@@ -28,6 +28,7 @@ BANK = 512
 ROW_TILES = BANK // P
 BANKS = BLOCK // BANK
 LN_EPS = 0.001
+WORK_BUFS = 4
 
 FLOPS = 2 * ROWS * (FEATURES + FEATURES * BASES) * UNITS
 
@@ -38,16 +39,12 @@ def tile_kanlinear_pa_t_kernel(
     nc = tc.nc
     with ExitStack() as ctx:
         const = ctx.enter_context(tc.tile_pool(name="const", bufs=1))
-        wprep = ctx.enter_context(tc.tile_pool(name="wprep", bufs=2))
         rows_pool = ctx.enter_context(tc.tile_pool(name="rows", bufs=2))
         small = ctx.enter_context(tc.tile_pool(name="small", bufs=2))
         xn_pool = ctx.enter_context(tc.tile_pool(name="xn", bufs=2))
-        work = ctx.enter_context(tc.tile_pool(name="work", bufs=3))
-        halves = ctx.enter_context(tc.tile_pool(name="halves", bufs=4))
         planes = ctx.enter_context(tc.tile_pool(name="planes", bufs=2))
         mx = ctx.enter_context(tc.tile_pool(name="mx", bufs=1))
-        psum_t = ctx.enter_context(tc.psum_pool(name="psum_t", bufs=4))
-        psum_o = ctx.enter_context(tc.psum_pool(name="psum_o", bufs=4))
+        psum = ctx.enter_context(tc.psum_pool(name="psum", bufs=8))
 
         ident = const.tile([P, P], F32)
         make_identity(nc, ident[:])
@@ -102,18 +99,21 @@ def tile_kanlinear_pa_t_kernel(
         nc.vector.tensor_scalar_mul(out=neg_mu[:], in0=neg_mu[:], scalar1=-1.0)
 
 
-        w_raw = wprep.tile([P, PASSES * PACK, UNITS], BF16, bufs=1)
-        nc.scalar.dma_start(out=w_raw[:, 0:PACK, :], in_=base_weight.rearrange("(t p) u -> p t u", p=P))
-        nc.scalar.dma_start(
-            out=w_raw[:, PACK:, :].rearrange("p (c j) u -> p c (j u)", j=BASES),
-            in_=spline_weight.rearrange("(c p j) u -> p c (j u)", p=P, j=BASES),
-        )
         w_codes = const.tile([P, PASSES, UNITS], U32, align_bytes=64)
         w_scales = const.tile([P, PASSES, UNITS], U8, align_bytes=64)
 
-        def quantise_weights():
+        def load_weights(pool):
+            w_raw = pool.tile([P, PASSES * PACK, UNITS], BF16, bufs=1)
+            nc.scalar.dma_start(out=w_raw[:, 0:PACK, :], in_=base_weight.rearrange("(t p) u -> p t u", p=P))
+            nc.scalar.dma_start(
+                out=w_raw[:, PACK:, :].rearrange("p (c j) u -> p c (j u)", j=BASES),
+                in_=spline_weight.rearrange("(c p j) u -> p c (j u)", p=P, j=BASES),
+            )
+            return w_raw
+
+        def quantise_weights(pool, w_raw):
             for k in range(PASSES):
-                w_grouped = wprep.tile([P, UNITS, PACK], BF16, align_bytes=64)
+                w_grouped = pool.tile([P, UNITS, PACK], BF16, align_bytes=64)
                 nc.vector.tensor_copy(
                     out=w_grouped[:], in_=w_raw[:, k * PACK : (k + 1) * PACK, :].rearrange("p t u -> p u t")
                 )
@@ -129,6 +129,7 @@ def tile_kanlinear_pa_t_kernel(
         x_sb, row_scale, row_shift, z_t, xn = {}, {}, {}, {}, {}
         square, cube, up, down = {}, {}, {}, {}
         left, right, grouped, codes, scales, acc = {}, {}, {}, {}, {}, {}
+        pools = {}
 
         def load_rows(bank):
             x_sb[bank] = rows_pool.tile([P, ROW_TILES, FEATURES], BF16, name="x_sb")
@@ -157,7 +158,7 @@ def tile_kanlinear_pa_t_kernel(
                     scale=row_scale[bank][:, t : t + 1], bias=row_shift[bank][:, t : t + 1],
                 )
             for c in range(CHUNKS):
-                z_t[bank, c] = psum_t.tile([P, BANK], F32, name="z_t")
+                z_t[bank, c] = psum.tile([P, BANK], F32, name="z_t", tag="bank")
                 for t in range(ROW_TILES):
                     nc.tensor.transpose(
                         z_t[bank, c][:, t * P : (t + 1) * P], z[:, t, c * P : (c + 1) * P], ident[:]
@@ -190,14 +191,14 @@ def tile_kanlinear_pa_t_kernel(
 
         def square_of(s):
             b, c, i = steps[s]
-            square[s] = work.tile([P, BLOCK], F32, name="square")
+            square[s] = pools["work"].tile([P, BLOCK], F32, name="square")
             nc.scalar.activation(
                 out=square[s][:], in_=xn[b][:, c, :], func=ACT.Square, bias=neg_knots[:, c, i : i + 1]
             )
 
         def cube_of(s):
             b, c, i = steps[s]
-            cube[s] = work.tile([P, BLOCK], F32, name="cube")
+            cube[s] = pools["work"].tile([P, BLOCK], F32, name="cube")
             nc.vector.scalar_tensor_tensor(
                 out=cube[s][:], in0=xn[b][:, c, :], scalar=knots[:, c, i : i + 1], in1=square[s][:],
                 op0=ALU.subtract, op1=ALU.mult,
@@ -206,10 +207,10 @@ def tile_kanlinear_pa_t_kernel(
         def halves_of(s):
             b, c, i = steps[s]
             if i <= 6:
-                up[s] = halves.tile([P, BLOCK], F32, name="up")
+                up[s] = pools["work"].tile([P, BLOCK], F32, name="up")
                 nc.scalar.activation(out=up[s][:], in_=cube[s][:], func=ACT.Relu, scale=rise[:, c, i : i + 1])
             if i >= 3:
-                down[s] = halves.tile([P, BLOCK], F32, name="down")
+                down[s] = pools["work"].tile([P, BLOCK], F32, name="down")
                 nc.scalar.activation(
                     out=down[s][:], in_=cube[s][:], func=ACT.Relu, scale=neg_fall[:, c, i - 3 : i - 2]
                 )
@@ -258,38 +259,40 @@ def tile_kanlinear_pa_t_kernel(
                 dst = grouped[b, group][:].rearrange("p (a i) t -> p a t i", i=4)
                 src = left[b, group][:].rearrange("p t (a i) -> p a t i", i=4)
                 if group % 2 == 0:
-                    nc.vector.tensor_copy(out=dst, in_=src)
-                else:
                     nc.scalar.copy(out=dst, in_=src)
+                else:
+                    nc.vector.tensor_copy(out=dst, in_=src)
 
         def quantise_at(s):
             group = group_done_at(s)
             if group is not None:
                 quantise(steps[s][0], group, 1 + group)
 
-        def multiply(bank):
-            b, h = divmod(bank, BANKS)
-            for t in range(ROW_TILES):
-                cols = slice((h * ROW_TILES + t) * P, (h * ROW_TILES + t + 1) * P)
-                acc[bank, t] = psum_o.tile([P, UNITS], F32, name="acc")
-                for k in range(PASSES):
+        BLOCK_TILES = BLOCK // P
+
+        def multiply(b, passes):
+            for t in range(BLOCK_TILES):
+                cols = slice(t * P, (t + 1) * P)
+                if passes[0] == 0:
+                    acc[b, t] = psum.tile([P, UNITS], F32, name="acc", tag="bank")
+                for k in passes:
                     nc.tensor.matmul_mx(
-                        out=acc[bank, t][:],
+                        out=acc[b, t][:],
                         lhsT=codes[b][:, k, cols].bitcast(FP8X4), lhsT_scale=scales[b][:, k, cols],
                         rhs=w_codes[:, k, :].bitcast(FP8X4), rhs_scale=w_scales[:, k, :],
                         start=(k == 0), stop=(k == PASSES - 1),
                     )
 
-        def add_bias_and_store(bank):
+        def add_bias_and_store(b, h):
             result = rows_pool.tile([P, ROW_TILES, UNITS], F32)
             for t in range(ROW_TILES):
-                nc.vector.tensor_add(out=result[:, t, :], in0=acc[bank, t][:], in1=bias[:])
-            nc.sync.dma_start(out=out_banks[bank], in_=result[:])
+                nc.vector.tensor_add(out=result[:, t, :], in0=acc[b, h * ROW_TILES + t][:], in1=bias[:])
+            nc.sync.dma_start(out=out_banks[b * BANKS + h], in_=result[:])
 
         def side_jobs(s):
             b, c, i = steps[s]
-            if c < BANKS and b + 1 < BLOCKS:
-                bank = (b + 1) * BANKS + c
+            if 1 <= c <= BANKS and b + 1 < BLOCKS:
+                bank = (b + 1) * BANKS + c - 1
                 if i == 0:
                     load_rows(bank)
                 if i == 3:
@@ -298,35 +301,42 @@ def tile_kanlinear_pa_t_kernel(
                     normalise_and_transpose(bank)
                 if i == 7:
                     gamma_beta(bank)
-            if c == 2 and i == 0:
+            if c == CHUNKS - 1 and i == 0:
                 relu_branch(b)
-            if c == 2 and i == 2:
+            if c == CHUNKS - 1 and i == 2:
                 quantise(b, "relu", 0)
 
-        def products_after(s):
-            b, c, i = steps[s]
-            return b if (c == CHUNKS - 1 and i == KNOTS - 1) else None
+        def products_at(s, lag):
+            b = steps[s][0]
+            group = group_done_at(s)
+            if group == SPLINE_PASSES - 2 and lag == 1:
+                multiply(b, list(range(PASSES - 1)))
+            if group == SPLINE_PASSES - 1 and lag == 1:
+                multiply(b, [PASSES - 1])
+            if group == SPLINE_PASSES - 1 and lag == 2:
+                for h in range(BANKS):
+                    add_bias_and_store(b, h)
 
         for bank in range(BANKS):
             load_rows(bank)
-        for bank in range(BANKS):
-            row_statistics(bank)
-        quantise_weights()
+        with tc.tile_pool(name="wprep", bufs=2) as wprep:
+            w_raw = load_weights(wprep)
+            for bank in range(BANKS):
+                row_statistics(bank)
+            quantise_weights(wprep, w_raw)
+        pools["work"] = ctx.enter_context(tc.tile_pool(name="work", bufs=WORK_BUFS, reuse_waits="tile"))
         for bank in range(BANKS):
             normalise_and_transpose(bank)
             gamma_beta(bank)
 
         stages = (square_of, cube_of, halves_of, forms_of, regroup_at, quantise_at)
-        for r in range(len(steps) + len(stages) + BANKS):
+        for r in range(len(steps) + len(stages) + 2):
             if r < len(steps):
                 side_jobs(r)
             for lag, stage in enumerate(stages):
                 if 0 <= r - lag < len(steps):
                     stage(r - lag)
-            for h in range(BANKS):
-                s = r - len(stages) - h
-                if 0 <= s < len(steps) and products_after(s) is not None:
-                    multiply(products_after(s) * BANKS + h)
-                s = s - 1
-                if 0 <= s < len(steps) and products_after(s) is not None:
-                    add_bias_and_store(products_after(s) * BANKS + h)
+            for lag in (1, 2):
+                s = r - (len(stages) - 1) - lag
+                if 0 <= s < len(steps):
+                    products_at(s, lag)

@@ -19,16 +19,17 @@ UNITS = 256
 KNOTS = 10
 BASES = 6
 CHUNKS = FEATURES // P
-PLANES = CHUNKS * BASES
-SPLINE_PASSES = PLANES // PACK
+PAIRS = BASES // 2
+HALF_P = P // 2
+SPLINE_PASSES = CHUNKS * PAIRS // 2
 PASSES = 1 + SPLINE_PASSES
 BLOCK = 1024
 BLOCKS = ROWS // BLOCK
 BANK = 512
-ROW_TILES = BANK // P
+TILES = BANK // P
 BANKS = BLOCK // BANK
 LN_EPS = 0.001
-WORK_BUFS = 4
+SCALAR_TERMS = (0, 1, 2)
 
 FLOPS = 2 * ROWS * (FEATURES + FEATURES * BASES) * UNITS
 
@@ -43,8 +44,8 @@ def tile_kanlinear_pa_t_kernel(
         small = ctx.enter_context(tc.tile_pool(name="small", bufs=2))
         xn_pool = ctx.enter_context(tc.tile_pool(name="xn", bufs=2))
         planes = ctx.enter_context(tc.tile_pool(name="planes", bufs=2))
-        mx = ctx.enter_context(tc.tile_pool(name="mx", bufs=1))
-        psum = ctx.enter_context(tc.psum_pool(name="psum", bufs=8))
+        mx = ctx.enter_context(tc.tile_pool(name="mx", bufs=2))
+        psum = ctx.enter_context(tc.psum_pool(name="psum", bufs=2))
 
         ident = const.tile([P, P], F32)
         make_identity(nc, ident[:])
@@ -61,15 +62,18 @@ def tile_kanlinear_pa_t_kernel(
 
         gamma = const.tile([P, CHUNKS], F32)
         beta = const.tile([P, CHUNKS], F32)
-        bias = const.tile([P, UNITS], F32)
+        bias = const.tile([P, 2, UNITS], F32)
         knots = const.tile([P, CHUNKS, KNOTS], F32)
         nc.vector.tensor_copy(out=gamma[:], in_=gamma_bf[:])
         nc.vector.tensor_copy(out=beta[:], in_=beta_bf[:])
-        nc.vector.tensor_copy(out=bias[:], in_=bias_bf[:])
+        nc.vector.tensor_copy(out=bias[:, 0, :], in_=bias_bf[:])
+        nc.vector.tensor_copy(out=bias[:, 1, :], in_=bias_bf[:])
         nc.vector.tensor_copy(out=knots[:], in_=knots_bf[:])
         neg_knots = const.tile([P, CHUNKS, KNOTS], F32)
         nc.vector.tensor_scalar_mul(out=neg_knots[:], in0=knots[:], scalar1=-1.0)
-        neg_half = const.tile([P, ROW_TILES], F32)
+        half = const.tile([P, CHUNKS, KNOTS], F32)
+        nc.vector.memset(half[:], 0.5)
+        neg_half = const.tile([P, TILES], F32)
         nc.vector.memset(neg_half[:], -0.5)
 
         span = {}
@@ -80,24 +84,36 @@ def tile_kanlinear_pa_t_kernel(
         nc.vector.reciprocal(out=inv_span1[:], in_=span[1][:])
 
         ENDS = KNOTS - 3
+        inv_rise = const.tile([P, CHUNKS, ENDS], F32)
+        inv_fall = const.tile([P, CHUNKS, ENDS], F32)
         rise = const.tile([P, CHUNKS, ENDS], F32)
-        neg_fall = const.tile([P, CHUNKS, ENDS], F32)
-        prod = const.tile([P, CHUNKS, ENDS], F32)
-        nc.vector.tensor_mul(out=prod[:], in0=span[1][:, :, 0:ENDS], in1=span[2][:, :, 0:ENDS])
-        nc.vector.tensor_mul(out=prod[:], in0=prod[:], in1=span[3][:])
-        nc.vector.reciprocal(out=rise[:], in_=prod[:])
-        prod2 = const.tile([P, CHUNKS, ENDS], F32)
-        nc.vector.tensor_mul(out=prod2[:], in0=span[1][:, :, 2 : 2 + ENDS], in1=span[2][:, :, 1 : 1 + ENDS])
-        nc.vector.tensor_mul(out=prod2[:], in0=prod2[:], in1=span[3][:])
-        nc.vector.reciprocal(out=neg_fall[:], in_=prod2[:])
-        nc.vector.tensor_scalar_mul(out=neg_fall[:], in0=neg_fall[:], scalar1=-1.0)
-        neg_lam = const.tile([P, CHUNKS, BASES], F32)
-        neg_mu = const.tile([P, CHUNKS, BASES], F32)
-        nc.vector.tensor_mul(out=neg_lam[:], in0=span[4][:], in1=inv_span1[:, :, 0:BASES])
-        nc.vector.tensor_scalar_mul(out=neg_lam[:], in0=neg_lam[:], scalar1=-1.0)
-        nc.vector.tensor_mul(out=neg_mu[:], in0=span[4][:], in1=inv_span1[:, :, 3 : 3 + BASES])
-        nc.vector.tensor_scalar_mul(out=neg_mu[:], in0=neg_mu[:], scalar1=-1.0)
+        fall = const.tile([P, CHUNKS, ENDS], F32)
+        nc.vector.tensor_mul(out=inv_rise[:], in0=span[1][:, :, 0:ENDS], in1=span[2][:, :, 0:ENDS])
+        nc.vector.tensor_mul(out=inv_rise[:], in0=inv_rise[:], in1=span[3][:])
+        nc.vector.reciprocal(out=rise[:], in_=inv_rise[:])
+        nc.vector.tensor_mul(out=inv_fall[:], in0=span[1][:, :, 2 : 2 + ENDS], in1=span[2][:, :, 1 : 1 + ENDS])
+        nc.vector.tensor_mul(out=inv_fall[:], in0=inv_fall[:], in1=span[3][:])
+        nc.vector.reciprocal(out=fall[:], in_=inv_fall[:])
 
+        lead = const.tile([P, CHUNKS, KNOTS], F32)
+        nc.vector.tensor_copy(out=lead[:, :, 0:6], in_=rise[:, :, 0:6])
+        nc.vector.tensor_copy(out=lead[:, :, 6:10], in_=fall[:, :, 3:7])
+        root = const.tile([P, CHUNKS, KNOTS], F32)
+        nc.gpsimd.tensor_tensor(out=root[:], in0=lead[:], in1=half[:], op=ALU.pow)
+        root_shift = const.tile([P, CHUNKS, KNOTS], F32)
+        nc.vector.tensor_mul(out=root_shift[:], in0=root[:], in1=neg_knots[:])
+        swap = const.tile([P, CHUNKS, 3], F32)
+        nc.vector.tensor_mul(out=swap[:], in0=inv_rise[:, :, 3:6], in1=fall[:, :, 0:3])
+        swap_back = const.tile([P, CHUNKS, 1], F32)
+        nc.vector.tensor_mul(out=swap_back[:], in0=inv_fall[:, :, 3:4], in1=rise[:, :, 6:7])
+        left_second = const.tile([P, CHUNKS, BASES], F32)
+        right_second = const.tile([P, CHUNKS, BASES], F32)
+        nc.vector.tensor_mul(out=left_second[:], in0=span[4][:], in1=inv_span1[:, :, 0:BASES])
+        nc.vector.tensor_scalar_mul(out=left_second[:], in0=left_second[:], scalar1=-1.0)
+        nc.vector.tensor_mul(out=left_second[:, :, 5:6], in0=left_second[:, :, 5:6], in1=swap_back[:])
+        nc.vector.tensor_mul(out=right_second[:], in0=span[4][:], in1=inv_span1[:, :, 3 : 3 + BASES])
+        nc.vector.tensor_scalar_mul(out=right_second[:], in0=right_second[:], scalar1=-1.0)
+        nc.vector.tensor_mul(out=right_second[:, :, 0:3], in0=right_second[:, :, 0:3], in1=swap[:])
 
         w_codes = const.tile([P, PASSES, UNITS], U32, align_bytes=64)
         w_scales = const.tile([P, PASSES, UNITS], U8, align_bytes=64)
@@ -105,10 +121,15 @@ def tile_kanlinear_pa_t_kernel(
         def load_weights(pool):
             w_raw = pool.tile([P, PASSES * PACK, UNITS], BF16, bufs=1)
             nc.scalar.dma_start(out=w_raw[:, 0:PACK, :], in_=base_weight.rearrange("(t p) u -> p t u", p=P))
-            nc.scalar.dma_start(
-                out=w_raw[:, PACK:, :].rearrange("p (c j) u -> p c (j u)", j=BASES),
-                in_=spline_weight.rearrange("(c p j) u -> p c (j u)", p=P, j=BASES),
-            )
+            by_plane = spline_weight.rearrange("(c m e k o) u -> c o e m k u", c=CHUNKS, e=2, k=PAIRS, o=2)
+            for c in range(CHUNKS):
+                for o in range(2):
+                    for e in range(2):
+                        first = PACK + 2 * PAIRS * c + e
+                        nc.scalar.dma_start(
+                            out=w_raw[o * HALF_P : (o + 1) * HALF_P, first : first + 2 * PAIRS - 1 : 2, :],
+                            in_=by_plane[c, o, e],
+                        )
             return w_raw
 
         def quantise_weights(pool, w_raw):
@@ -123,171 +144,203 @@ def tile_kanlinear_pa_t_kernel(
                     in_=w_grouped[:].rearrange("p u t -> p (u t)"),
                 )
 
-        x_banks = x.rearrange("(b t p) f -> b p t f", t=ROW_TILES, p=P)
-        out_banks = out.rearrange("(b t p) u -> b p t u", t=ROW_TILES, p=P)
+        x_banks = x.rearrange("(b t p) f -> b p t f", t=TILES, p=P)
+        out_banks = out.rearrange("(b t p) u -> b p t u", t=TILES, p=P)
 
         x_sb, row_scale, row_shift, z_t, xn = {}, {}, {}, {}, {}
-        square, cube, up, down = {}, {}, {}, {}
-        left, right, grouped, codes, scales, acc = {}, {}, {}, {}, {}, {}
+        square, cube, left_term, right_term, right_lead = {}, {}, {}, {}, {}
+        left, right, left_bf, basis, back, grouped, codes, scales = {}, {}, {}, {}, {}, {}, {}, {}
         pools = {}
 
         def load_rows(bank):
-            x_sb[bank] = rows_pool.tile([P, ROW_TILES, FEATURES], BF16, name="x_sb")
+            x_sb[bank] = rows_pool.tile([P, TILES, FEATURES], BF16, name="x_sb")
             nc.sync.dma_start(out=x_sb[bank][:], in_=x_banks[bank])
 
         def row_statistics(bank):
-            stats = small.tile([P, ROW_TILES, 6], F32)
-            mean_var = small.tile([P, ROW_TILES, 2], F32)
-            for t in range(ROW_TILES):
+            stats = small.tile([P, TILES, 6], F32)
+            mean_var = small.tile([P, TILES, 2], F32)
+            for t in range(TILES):
                 nc.vector.bn_stats(out=stats[:, t, :], in_=x_sb[bank][:, t, :])
                 nc.vector.bn_aggr(out=mean_var[:, t, :], in_=stats[:, t, :])
-            var_eps = small.tile([P, ROW_TILES], F32)
+            var_eps = small.tile([P, TILES], F32)
             nc.vector.tensor_scalar_add(out=var_eps[:], in0=mean_var[:, :, 1], scalar1=LN_EPS)
-            neg_mean = small.tile([P, ROW_TILES], F32)
+            neg_mean = small.tile([P, TILES], F32)
             nc.vector.tensor_scalar_mul(out=neg_mean[:], in0=mean_var[:, :, 0], scalar1=-1.0)
-            row_scale[bank] = small.tile([P, ROW_TILES], F32, name="row_scale")
+            row_scale[bank] = small.tile([P, TILES], F32, name="row_scale")
             nc.gpsimd.tensor_tensor(out=row_scale[bank][:], in0=var_eps[:], in1=neg_half[:], op=ALU.pow)
-            row_shift[bank] = small.tile([P, ROW_TILES], F32, name="row_shift")
+            row_shift[bank] = small.tile([P, TILES], F32, name="row_shift")
             nc.gpsimd.tensor_tensor(out=row_shift[bank][:], in0=neg_mean[:], in1=row_scale[bank][:], op=ALU.mult)
 
         def normalise_and_transpose(bank):
-            z = rows_pool.tile([P, ROW_TILES, FEATURES], F32, bufs=1)
-            for t in range(ROW_TILES):
+            z = rows_pool.tile([P, TILES, FEATURES], F32, bufs=1)
+            for t in range(TILES):
                 nc.scalar.activation(
                     out=z[:, t, :], in_=x_sb[bank][:, t, :], func=ACT.Identity,
                     scale=row_scale[bank][:, t : t + 1], bias=row_shift[bank][:, t : t + 1],
                 )
-            for c in range(CHUNKS):
-                z_t[bank, c] = psum.tile([P, BANK], F32, name="z_t", tag="bank")
-                for t in range(ROW_TILES):
-                    nc.tensor.transpose(
-                        z_t[bank, c][:, t * P : (t + 1) * P], z[:, t, c * P : (c + 1) * P], ident[:]
-                    )
-
-        def gamma_beta(bank):
             b, h = divmod(bank, BANKS)
             if h == 0:
                 xn[b] = xn_pool.tile([P, CHUNKS, BLOCK], F32, name="xn")
             for c in range(CHUNKS):
+                z_t = psum.tile([P, BANK], F32, name="z_t", tag="misc")
+                for t in range(TILES):
+                    nc.tensor.transpose(z_t[:, t * P : (t + 1) * P], z[:, t, c * P : (c + 1) * P], ident[:])
                 nc.scalar.activation(
-                    out=xn[b][:, c, h * BANK : (h + 1) * BANK], in_=z_t[bank, c][:], func=ACT.Identity,
+                    out=xn[b][:, c, h * BANK : (h + 1) * BANK], in_=z_t[:], func=ACT.Identity,
                     scale=gamma[:, c : c + 1], bias=beta[:, c : c + 1],
                 )
 
-        def relu_branch(b):
-            grouped[b, "relu"] = planes.tile([P, BLOCK, PACK], BF16, align_bytes=64, name="grouped")
-            nc.scalar.activation(out=grouped[b, "relu"][:], in_=xn[b][:].rearrange("p t n -> p n t"), func=ACT.Relu)
+        def relu_branch(b, h):
+            grouped[b, h, 0] = planes.tile([P, BANK, PACK], BF16, align_bytes=64, name="grouped", bufs=6)
+            nc.scalar.activation(
+                out=grouped[b, h, 0][:],
+                in_=xn[b][:, :, h * BANK : (h + 1) * BANK].rearrange("p t n -> p n t"), func=ACT.Relu,
+            )
 
-        def quantise(b, key, k):
-            if b not in codes:
-                codes[b] = mx.tile([P, PASSES, BLOCK], U32, align_bytes=64, name="codes")
-                scales[b] = mx.tile([P, PASSES, BLOCK], U8, align_bytes=64, name="scales")
+        def quantise(b, h, k):
+            if (b, h) not in codes:
+                codes[b, h] = mx.tile([P, PASSES, BANK], U32, align_bytes=64, name="codes")
+                scales[b, h] = mx.tile([P, PASSES, BANK], U8, align_bytes=64, name="scales")
             nc.vector.quantize_mx(
-                out=codes[b][:, k, :].bitcast(FP8X4), scales=scales[b][:, k, :],
-                in_=grouped[b, key][:].rearrange("p n t -> p (n t)"),
+                out=codes[b, h][:, k, :].bitcast(FP8X4), scales=scales[b, h][:, k, :],
+                in_=grouped[b, h, k][:].rearrange("p n t -> p (n t)"),
             )
 
         steps = [(b, c, i) for b in range(BLOCKS) for c in range(CHUNKS) for i in range(KNOTS)]
 
         def square_of(s):
             b, c, i = steps[s]
-            square[s] = pools["work"].tile([P, BLOCK], F32, name="square")
+            square[s] = pools["work"].tile([P, BLOCK], F32, name="square", bufs=3)
             nc.scalar.activation(
-                out=square[s][:], in_=xn[b][:, c, :], func=ACT.Square, bias=neg_knots[:, c, i : i + 1]
+                out=square[s][:], in_=xn[b][:, c, :], func=ACT.Square,
+                scale=root[:, c, i : i + 1], bias=root_shift[:, c, i : i + 1],
             )
 
         def cube_of(s):
             b, c, i = steps[s]
-            cube[s] = pools["work"].tile([P, BLOCK], F32, name="cube")
+            cube[s] = pools["work"].tile([P, BLOCK], F32, name="cube", bufs=6)
             nc.vector.scalar_tensor_tensor(
                 out=cube[s][:], in0=xn[b][:, c, :], scalar=knots[:, c, i : i + 1], in1=square[s][:],
                 op0=ALU.subtract, op1=ALU.mult,
             )
 
-        def halves_of(s):
-            b, c, i = steps[s]
-            if i <= 6:
-                up[s] = pools["work"].tile([P, BLOCK], F32, name="up")
-                nc.scalar.activation(out=up[s][:], in_=cube[s][:], func=ACT.Relu, scale=rise[:, c, i : i + 1])
-            if i >= 3:
-                down[s] = pools["work"].tile([P, BLOCK], F32, name="down")
-                nc.scalar.activation(
-                    out=down[s][:], in_=cube[s][:], func=ACT.Relu, scale=neg_fall[:, c, i - 3 : i - 2]
-                )
-
-        def group_done_at(s):
-            b, c, i = steps[s]
-            if i < 4:
-                return None
-            group, slot = divmod(c * BASES + i - 4, PACK)
-            return group if slot == PACK - 1 else None
-
-        def forms_of(s):
+        def terms_of(s):
             b, c, i = steps[s]
             if 1 <= i <= 6:
                 j = i - 1
-                group, slot = divmod(c * BASES + j, PACK)
-                if slot == 0:
-                    left[b, group] = planes.tile([P, PACK, BLOCK], BF16, name="left")
-                nc.vector.scalar_tensor_tensor(
-                    out=left[b, group][:, slot, :], in0=up[s][:], scalar=neg_lam[:, c, j : j + 1],
-                    in1=up[s - 1][:], op0=ALU.mult, op1=ALU.add,
+                left_term[s] = pools["work"].tile([P, BLOCK], F32, name="left_term", bufs=2)
+                nc.vector.tensor_scalar(
+                    out=left_term[s][:], in0=cube[s][:], scalar1=0.0, scalar2=left_second[:, c, j : j + 1],
+                    op0=ALU.max, op1=ALU.mult,
                 )
-            if i >= 4:
-                j = i - 4
-                group, slot = divmod(c * BASES + j, PACK)
-                if slot == 0:
-                    right[b, group] = planes.tile([P, PACK, BLOCK], BF16, name="right")
-                nc.vector.scalar_tensor_tensor(
-                    out=right[b, group][:, slot, :], in0=down[s - 1][:], scalar=neg_mu[:, c, j : j + 1],
-                    in1=down[s][:], op0=ALU.mult, op1=ALU.add,
-                )
-            group = group_done_at(s)
-            if group is not None:
-                nc.vector.tensor_tensor(
-                    out=left[b, group][:].rearrange("p t n -> p (t n)"),
-                    in0=left[b, group][:].rearrange("p t n -> p (t n)"),
-                    in1=right[b, group][:].rearrange("p t n -> p (t n)"),
-                    op=ALU.max,
-                )
-
-        def regroup_at(s):
-            b = steps[s][0]
-            group = group_done_at(s)
-            if group is not None:
-                grouped[b, group] = planes.tile([P, BLOCK, PACK], BF16, align_bytes=64, name="grouped")
-                dst = grouped[b, group][:].rearrange("p (a i) t -> p a t i", i=4)
-                src = left[b, group][:].rearrange("p t (a i) -> p a t i", i=4)
-                if group % 2 == 0:
-                    nc.scalar.copy(out=dst, in_=src)
+            if 3 <= i <= 8:
+                j = i - 3
+                right_term[s] = pools["work"].tile([P, BLOCK], F32, name="right_term", bufs=3)
+                if j in SCALAR_TERMS:
+                    nc.scalar.activation(
+                        out=right_term[s][:], in_=cube[s][:], func=ACT.Relu, scale=right_second[:, c, j : j + 1]
+                    )
                 else:
-                    nc.vector.tensor_copy(out=dst, in_=src)
+                    nc.vector.tensor_scalar(
+                        out=right_term[s][:], in0=cube[s][:], scalar1=0.0, scalar2=right_second[:, c, j : j + 1],
+                        op0=ALU.min, op1=ALU.mult,
+                    )
+            if 4 <= i <= 5:
+                right_lead[s] = pools["work"].tile([P, BLOCK], F32, name="right_lead", bufs=2)
+                nc.vector.tensor_scalar_mul(
+                    out=right_lead[s][:], in0=cube[s][:], scalar1=swap[:, c, i - 3 : i - 2]
+                )
 
-        def quantise_at(s):
-            group = group_done_at(s)
-            if group is not None:
-                quantise(steps[s][0], group, 1 + group)
-
-        BLOCK_TILES = BLOCK // P
-
-        def multiply(b, passes):
-            for t in range(BLOCK_TILES):
-                cols = slice(t * P, (t + 1) * P)
-                if passes[0] == 0:
-                    acc[b, t] = psum.tile([P, UNITS], F32, name="acc", tag="bank")
-                for k in passes:
-                    nc.tensor.matmul_mx(
-                        out=acc[b, t][:],
-                        lhsT=codes[b][:, k, cols].bitcast(FP8X4), lhsT_scale=scales[b][:, k, cols],
-                        rhs=w_codes[:, k, :].bitcast(FP8X4), rhs_scale=w_scales[:, k, :],
-                        start=(k == 0), stop=(k == PASSES - 1),
+        def add_up(bank, first, second, h):
+            for t in range(TILES):
+                rows = slice(h * BANK + t * P, h * BANK + (t + 1) * P)
+                for term, start in ((first, True), (second, False)):
+                    nc.tensor.matmul(
+                        bank[:, t * P : (t + 1) * P], lhsT=term[:, rows], rhs=ident[:],
+                        is_transpose=True, start=start, stop=not start,
                     )
 
-        def add_bias_and_store(b, h):
-            result = rows_pool.tile([P, ROW_TILES, UNITS], F32)
-            for t in range(ROW_TILES):
-                nc.vector.tensor_add(out=result[:, t, :], in0=acc[b, h * ROW_TILES + t][:], in1=bias[:])
-            nc.sync.dma_start(out=out_banks[b * BANKS + h], in_=result[:])
+        def forms_of(s):
+            b, c, i = steps[s]
+            for h in range(BANKS):
+                if 1 <= i <= 6:
+                    left[s, h] = psum.tile([P, BANK], F32, name="left", tag="left")
+                    add_up(left[s, h], cube[s - 1], left_term[s], h)
+                if i >= 4:
+                    right[s, h] = psum.tile([P, BANK], F32, name="right", tag="right")
+                    add_up(right[s, h], right_lead[s] if i <= 5 else cube[s], right_term[s - 1], h)
+
+        def reads_of(s):
+            b, c, i = steps[s]
+            for h in range(BANKS):
+                if 1 <= i <= 6:
+                    j = i - 1
+                    left_bf[b, c, j, h] = planes.tile([P, BANK], BF16, name="left_bf", bufs=12)
+                    nc.scalar.activation(out=left_bf[b, c, j, h][:], in_=left[s, h][:], func=ACT.Relu)
+                if i >= 4:
+                    j = i - 4
+                    if j == 0 and h == 0:
+                        basis[b, c] = planes.tile([P, BANKS, TILES, BASES, P], BF16, name="basis")
+                    nc.vector.scalar_tensor_tensor(
+                        out=basis[b, c][:, h, :, j, :], in0=right[s, h][:].rearrange("p (t f) -> p t f", f=P),
+                        scalar=-1.0, in1=left_bf[b, c, j, h][:].rearrange("p (t f) -> p t f", f=P),
+                        op0=ALU.mult, op1=ALU.max,
+                    )
+
+        def pass_done_at(s):
+            b, c, i = steps[s]
+            if i < 5 or i % 2 == 0:
+                return None
+            pair = c * PAIRS + (i - 5) // 2
+            return pair // 2 if pair % 2 == 1 else None
+
+        def transpose_back(s):
+            k = pass_done_at(s)
+            if k is None:
+                return
+            b = steps[s][0]
+            for h in range(BANKS):
+                for a in range(TILES // 2):
+                    bank = psum.tile([P, 2, 2, P], F32, name="back", tag="back")
+                    for u in range(2):
+                        c, pair = divmod(2 * k + u, PAIRS)
+                        for t in range(2):
+                            words = basis[b, c][:, h, 2 * a + t, 2 * pair : 2 * pair + 2, :]
+                            nc.tensor.transpose(
+                                bank[:, u, t, :], words.rearrange("p j f -> p (j f)").bitcast(F32), ident[:]
+                            )
+                    if a == 0:
+                        grouped[b, h, 1 + k] = planes.tile([P, BANK, PACK], BF16, align_bytes=64, name="grouped", bufs=6)
+                    half_rows = BANK // 2
+                    dst = grouped[b, h, 1 + k][:].rearrange("p n t -> p (n t)").bitcast(F32)
+                    dst = dst[:, a * BANK : (a + 1) * BANK].rearrange("p (n u) -> p n u", u=2)
+                    nc.scalar.copy(out=dst, in_=bank[:].rearrange("p u t n -> p (t n) u"))
+
+        def quantise_at(s):
+            k = pass_done_at(s)
+            if k is not None:
+                for h in range(BANKS):
+                    quantise(steps[s][0], h, 1 + k)
+
+        def products_at(s):
+            b, c, i = steps[s]
+            if c < CHUNKS - 1 or i < KNOTS - 1:
+                return
+            for h in range(BANKS):
+                result = rows_pool.tile([P, TILES, UNITS], F32)
+                for a in range(TILES // 2):
+                    acc = psum.tile([P, 2, UNITS], F32, name="acc", tag="misc")
+                    for t in range(2):
+                        cols = slice((2 * a + t) * P, (2 * a + t + 1) * P)
+                        for k in range(PASSES):
+                            nc.tensor.matmul_mx(
+                                out=acc[:, t, :],
+                                lhsT=codes[b, h][:, k, cols].bitcast(FP8X4), lhsT_scale=scales[b, h][:, k, cols],
+                                rhs=w_codes[:, k, :].bitcast(FP8X4), rhs_scale=w_scales[:, k, :],
+                                start=(k == 0), stop=(k == PASSES - 1),
+                            )
+                    nc.vector.tensor_add(out=result[:, 2 * a : 2 * a + 2, :], in0=acc[:], in1=bias[:])
+                nc.sync.dma_start(out=out_banks[b * BANKS + h], in_=result[:])
 
         def side_jobs(s):
             b, c, i = steps[s]
@@ -297,25 +350,12 @@ def tile_kanlinear_pa_t_kernel(
                     load_rows(bank)
                 if i == 3:
                     row_statistics(bank)
-                if i == 5:
-                    normalise_and_transpose(bank)
                 if i == 7:
-                    gamma_beta(bank)
-            if c == CHUNKS - 1 and i == 0:
-                relu_branch(b)
-            if c == CHUNKS - 1 and i == 2:
-                quantise(b, "relu", 0)
-
-        def products_at(s, lag):
-            b = steps[s][0]
-            group = group_done_at(s)
-            if group == SPLINE_PASSES - 2 and lag == 1:
-                multiply(b, list(range(PASSES - 1)))
-            if group == SPLINE_PASSES - 1 and lag == 1:
-                multiply(b, [PASSES - 1])
-            if group == SPLINE_PASSES - 1 and lag == 2:
-                for h in range(BANKS):
-                    add_bias_and_store(b, h)
+                    normalise_and_transpose(bank)
+            if c == CHUNKS - 1 and i < BANKS:
+                relu_branch(b, i)
+            if c == CHUNKS - 1 and 2 <= i < 2 + BANKS:
+                quantise(b, i - 2, 0)
 
         for bank in range(BANKS):
             load_rows(bank)
@@ -324,19 +364,14 @@ def tile_kanlinear_pa_t_kernel(
             for bank in range(BANKS):
                 row_statistics(bank)
             quantise_weights(wprep, w_raw)
-        pools["work"] = ctx.enter_context(tc.tile_pool(name="work", bufs=WORK_BUFS, reuse_waits="tile"))
+        pools["work"] = ctx.enter_context(tc.tile_pool(name="work", bufs=2, reuse_waits="tile"))
         for bank in range(BANKS):
             normalise_and_transpose(bank)
-            gamma_beta(bank)
 
-        stages = (square_of, cube_of, halves_of, forms_of, regroup_at, quantise_at)
-        for r in range(len(steps) + len(stages) + 2):
+        stages = (square_of, cube_of, terms_of, forms_of, reads_of, transpose_back, quantise_at, products_at)
+        for r in range(len(steps) + len(stages) - 1):
             if r < len(steps):
                 side_jobs(r)
             for lag, stage in enumerate(stages):
                 if 0 <= r - lag < len(steps):
                     stage(r - lag)
-            for lag in (1, 2):
-                s = r - (len(stages) - 1) - lag
-                if 0 <= s < len(steps):
-                    products_at(s, lag)

@@ -99,9 +99,7 @@ def tile_kanlinear_pa_t_kernel(
         nc.vector.tensor_copy(out=lead[:, :, 0:6], in_=rise[:, :, 0:6])
         nc.vector.tensor_copy(out=lead[:, :, 6:10], in_=fall[:, :, 3:7])
         root = const.tile([P, CHUNKS, KNOTS], F32)
-        nc.gpsimd.tensor_tensor(out=root[:], in0=lead[:], in1=half[:], op=ALU.pow)
         root_shift = const.tile([P, CHUNKS, KNOTS], F32)
-        nc.vector.tensor_mul(out=root_shift[:], in0=root[:], in1=neg_knots[:])
         swap = const.tile([P, CHUNKS, 3], F32)
         nc.vector.tensor_mul(out=swap[:], in0=inv_rise[:, :, 3:6], in1=fall[:, :, 0:3])
         swap_back = const.tile([P, CHUNKS, 1], F32)
@@ -147,10 +145,14 @@ def tile_kanlinear_pa_t_kernel(
         x_banks = x.rearrange("(b t p) f -> b p t f", t=TILES, p=P)
         out_banks = out.rearrange("(b t p) u -> b p t u", t=TILES, p=P)
 
-        x_sb, row_scale, row_shift, z_t, xn = {}, {}, {}, {}, {}
+        x_sb, row_scale, row_shift, z, z_t, xn = {}, {}, {}, {}, {}, {}
         square, cube, left_term, right_term, right_lead = {}, {}, {}, {}, {}
-        left, right, left_bf, basis, back, grouped, codes, scales = {}, {}, {}, {}, {}, {}, {}, {}
-        pools = {}
+        left, right, left_bf, basis, back, grouped = {}, {}, {}, {}, {}, {}
+        codes, scales, acc, result = {}, {}, {}, {}
+        pools, jobs = {}, {}
+
+        def roots_of(c):
+            nc.gpsimd.tensor_tensor(out=root[:, c, :], in0=lead[:, c, :], in1=half[:, c, :], op=ALU.pow)
 
         def load_rows(bank):
             x_sb[bank] = rows_pool.tile([P, TILES, FEATURES], BF16, name="x_sb")
@@ -161,6 +163,7 @@ def tile_kanlinear_pa_t_kernel(
             mean_var = small.tile([P, TILES, 2], F32)
             for t in range(TILES):
                 nc.vector.bn_stats(out=stats[:, t, :], in_=x_sb[bank][:, t, :])
+            for t in range(TILES):
                 nc.vector.bn_aggr(out=mean_var[:, t, :], in_=stats[:, t, :])
             var_eps = small.tile([P, TILES], F32)
             nc.vector.tensor_scalar_add(out=var_eps[:], in0=mean_var[:, :, 1], scalar1=LN_EPS)
@@ -171,24 +174,29 @@ def tile_kanlinear_pa_t_kernel(
             row_shift[bank] = small.tile([P, TILES], F32, name="row_shift")
             nc.gpsimd.tensor_tensor(out=row_shift[bank][:], in0=neg_mean[:], in1=row_scale[bank][:], op=ALU.mult)
 
-        def normalise_and_transpose(bank):
-            z = rows_pool.tile([P, TILES, FEATURES], F32, bufs=1)
+        def normalise(bank, t):
+            if t == 0:
+                z[bank] = rows_pool.tile([P, TILES, FEATURES], F32, name="z", bufs=1)
+            nc.scalar.activation(
+                out=z[bank][:, t, :], in_=x_sb[bank][:, t, :], func=ACT.Identity,
+                scale=row_scale[bank][:, t : t + 1], bias=row_shift[bank][:, t : t + 1],
+            )
+
+        def transpose_rows(bank, c):
+            z_t[bank, c] = psum.tile([P, BANK], F32, name="z_t", tag="misc")
             for t in range(TILES):
-                nc.scalar.activation(
-                    out=z[:, t, :], in_=x_sb[bank][:, t, :], func=ACT.Identity,
-                    scale=row_scale[bank][:, t : t + 1], bias=row_shift[bank][:, t : t + 1],
+                nc.tensor.transpose(
+                    z_t[bank, c][:, t * P : (t + 1) * P], z[bank][:, t, c * P : (c + 1) * P], ident[:]
                 )
+
+        def gamma_beta(bank, c):
             b, h = divmod(bank, BANKS)
-            if h == 0:
+            if h == 0 and c == 0:
                 xn[b] = xn_pool.tile([P, CHUNKS, BLOCK], F32, name="xn")
-            for c in range(CHUNKS):
-                z_t = psum.tile([P, BANK], F32, name="z_t", tag="misc")
-                for t in range(TILES):
-                    nc.tensor.transpose(z_t[:, t * P : (t + 1) * P], z[:, t, c * P : (c + 1) * P], ident[:])
-                nc.scalar.activation(
-                    out=xn[b][:, c, h * BANK : (h + 1) * BANK], in_=z_t[:], func=ACT.Identity,
-                    scale=gamma[:, c : c + 1], bias=beta[:, c : c + 1],
-                )
+            nc.scalar.activation(
+                out=xn[b][:, c, h * BANK : (h + 1) * BANK], in_=z_t[bank, c][:], func=ACT.Identity,
+                scale=gamma[:, c : c + 1], bias=beta[:, c : c + 1],
+            )
 
         def relu_branch(b, h):
             grouped[b, h, 0] = planes.tile([P, BANK, PACK], BF16, align_bytes=64, name="grouped", bufs=6)
@@ -206,26 +214,22 @@ def tile_kanlinear_pa_t_kernel(
                 in_=grouped[b, h, k][:].rearrange("p n t -> p (n t)"),
             )
 
-        steps = [(b, c, i) for b in range(BLOCKS) for c in range(CHUNKS) for i in range(KNOTS)]
-
-        def square_of(s):
-            b, c, i = steps[s]
-            square[s] = pools["work"].tile([P, BLOCK], F32, name="square", bufs=3)
+        def square_of(b, c, i):
+            square[b, c, i] = pools["work"].tile([P, BLOCK], F32, name="square", bufs=4)
             nc.scalar.activation(
-                out=square[s][:], in_=xn[b][:, c, :], func=ACT.Square,
+                out=square[b, c, i][:], in_=xn[b][:, c, :], func=ACT.Square,
                 scale=root[:, c, i : i + 1], bias=root_shift[:, c, i : i + 1],
             )
 
-        def cube_of(s):
-            b, c, i = steps[s]
-            cube[s] = pools["work"].tile([P, BLOCK], F32, name="cube", bufs=6)
+        def cube_of(b, c, i):
+            cube[b, c, i] = pools["work"].tile([P, BLOCK], F32, name="cube", bufs=6)
             nc.vector.scalar_tensor_tensor(
-                out=cube[s][:], in0=xn[b][:, c, :], scalar=knots[:, c, i : i + 1], in1=square[s][:],
+                out=cube[b, c, i][:], in0=xn[b][:, c, :], scalar=knots[:, c, i : i + 1], in1=square[b, c, i][:],
                 op0=ALU.subtract, op1=ALU.mult,
             )
 
-        def terms_of(s):
-            b, c, i = steps[s]
+        def terms_of(b, c, i):
+            s = (b, c, i)
             if 1 <= i <= 6:
                 j = i - 1
                 left_term[s] = pools["work"].tile([P, BLOCK], F32, name="left_term", bufs=2)
@@ -235,7 +239,7 @@ def tile_kanlinear_pa_t_kernel(
                 )
             if 3 <= i <= 8:
                 j = i - 3
-                right_term[s] = pools["work"].tile([P, BLOCK], F32, name="right_term", bufs=3)
+                right_term[s] = pools["work"].tile([P, BLOCK], F32, name="right_term", bufs=4)
                 if j in SCALAR_TERMS:
                     nc.scalar.activation(
                         out=right_term[s][:], in_=cube[s][:], func=ACT.Relu, scale=right_second[:, c, j : j + 1]
@@ -260,118 +264,147 @@ def tile_kanlinear_pa_t_kernel(
                         is_transpose=True, start=start, stop=not start,
                     )
 
-        def forms_of(s):
-            b, c, i = steps[s]
-            for h in range(BANKS):
-                if 1 <= i <= 6:
-                    left[s, h] = psum.tile([P, BANK], F32, name="left", tag="left")
-                    add_up(left[s, h], cube[s - 1], left_term[s], h)
-                if i >= 4:
-                    right[s, h] = psum.tile([P, BANK], F32, name="right", tag="right")
-                    add_up(right[s, h], right_lead[s] if i <= 5 else cube[s], right_term[s - 1], h)
+        def keep_clock(bank):
+            nc.tensor.matmul_mx(
+                out=bank[:],
+                lhsT=w_codes[:, 0, 0:P].bitcast(FP8X4), lhsT_scale=w_scales[:, 0, 0:P],
+                rhs=w_codes[:, 0:2, :].rearrange("p k u -> p (k u)").bitcast(FP8X4),
+                rhs_scale=w_scales[:, 0:2, :].rearrange("p k u -> p (k u)"),
+                start=True, stop=True,
+            )
 
-        def reads_of(s):
-            b, c, i = steps[s]
-            for h in range(BANKS):
-                if 1 <= i <= 6:
-                    j = i - 1
-                    left_bf[b, c, j, h] = planes.tile([P, BANK], BF16, name="left_bf", bufs=12)
-                    nc.scalar.activation(out=left_bf[b, c, j, h][:], in_=left[s, h][:], func=ACT.Relu)
-                if i >= 4:
-                    j = i - 4
-                    if j == 0 and h == 0:
-                        basis[b, c] = planes.tile([P, BANKS, TILES, BASES, P], BF16, name="basis")
-                    nc.vector.scalar_tensor_tensor(
-                        out=basis[b, c][:, h, :, j, :], in0=right[s, h][:].rearrange("p (t f) -> p t f", f=P),
-                        scalar=-1.0, in1=left_bf[b, c, j, h][:].rearrange("p (t f) -> p t f", f=P),
-                        op0=ALU.mult, op1=ALU.max,
+        def left_form(b, c, i, h):
+            left[b, c, i, h] = psum.tile([P, BANK], F32, name="left", tag="left")
+            keep_clock(left[b, c, i, h])
+            add_up(left[b, c, i, h], cube[b, c, i - 1], left_term[b, c, i], h)
+
+        def right_form(b, c, i, h):
+            right[b, c, i, h] = psum.tile([P, BANK], F32, name="right", tag="right")
+            first = right_lead[b, c, i] if i <= 5 else cube[b, c, i]
+            add_up(right[b, c, i, h], first, right_term[b, c, i - 1], h)
+
+        def read_left(b, c, i, h):
+            j = i - 1
+            left_bf[b, c, j, h] = planes.tile([P, BANK], BF16, name="left_bf", bufs=12)
+            nc.scalar.activation(out=left_bf[b, c, j, h][:], in_=left[b, c, i, h][:], func=ACT.Relu)
+
+        def larger_form(b, c, i, h):
+            j = i - 4
+            if j == 0 and h == 0:
+                basis[b, c] = planes.tile([P, BANKS, TILES, BASES, P], BF16, name="basis")
+            nc.vector.scalar_tensor_tensor(
+                out=basis[b, c][:, h, :, j, :], in0=right[b, c, i, h][:].rearrange("p (t f) -> p t f", f=P),
+                scalar=-1.0, in1=left_bf[b, c, j, h][:].rearrange("p (t f) -> p t f", f=P),
+                op0=ALU.mult, op1=ALU.max,
+            )
+
+        def transpose_back(b, k, h, a):
+            back[b, k, h, a] = psum.tile([P, 2, 2, P], F32, name="back", tag="back")
+            for u in range(2):
+                c, pair = divmod(2 * k + u, PAIRS)
+                for t in range(2):
+                    words = basis[b, c][:, h, 2 * a + t, 2 * pair : 2 * pair + 2, :]
+                    nc.tensor.transpose(
+                        back[b, k, h, a][:, u, t, :], words.rearrange("p j f -> p (j f)").bitcast(F32), ident[:]
                     )
 
-        def pass_done_at(s):
-            b, c, i = steps[s]
-            if i < 5 or i % 2 == 0:
-                return None
+        def regroup(b, k, h, a):
+            if a == 0:
+                grouped[b, h, 1 + k] = planes.tile([P, BANK, PACK], BF16, align_bytes=64, name="grouped", bufs=6)
+            dst = grouped[b, h, 1 + k][:].rearrange("p n t -> p (n t)").bitcast(F32)
+            dst = dst[:, a * BANK : (a + 1) * BANK].rearrange("p (n u) -> p n u", u=2)
+            nc.scalar.copy(out=dst, in_=back[b, k, h, a][:].rearrange("p u t n -> p (t n) u"))
+
+        def products(b, h, a):
+            acc[b, h, a] = psum.tile([P, 2, UNITS], F32, name="acc", tag="misc")
+            for t in range(2):
+                cols = slice((2 * a + t) * P, (2 * a + t + 1) * P)
+                for k in range(PASSES):
+                    nc.tensor.matmul_mx(
+                        out=acc[b, h, a][:, t, :],
+                        lhsT=codes[b, h][:, k, cols].bitcast(FP8X4), lhsT_scale=scales[b, h][:, k, cols],
+                        rhs=w_codes[:, k, :].bitcast(FP8X4), rhs_scale=w_scales[:, k, :],
+                        start=(k == 0), stop=(k == PASSES - 1),
+                    )
+
+        def add_bias(b, h, a):
+            if a == 0:
+                result[b, h] = rows_pool.tile([P, TILES, UNITS], F32, name="result")
+            nc.vector.tensor_add(out=result[b, h][:, 2 * a : 2 * a + 2, :], in0=acc[b, h, a][:], in1=bias[:])
+            if a == TILES // 2 - 1:
+                nc.sync.dma_start(out=out_banks[b * BANKS + h], in_=result[b, h][:])
+
+        HALF = KNOTS // 2
+        chunks = [(b, c) for b in range(BLOCKS) for c in range(CHUNKS)]
+        steps = []
+        for m in range(len(chunks) + 1):
+            for i in range(HALF):
+                if m < len(chunks):
+                    steps.append(chunks[m] + (i,))
+                if m > 0:
+                    steps.append(chunks[m - 1] + (i + HALF,))
+
+        def at(r, rank, job, args):
+            jobs.setdefault((r, rank), []).append((job, args))
+
+        for r, s in enumerate(steps):
+            b, c, i = s
+            at(r, 3, square_of, s)
+            at(r + 2, 1, cube_of, s)
+            at(r + 3, 2, terms_of, s)
+            for h in range(BANKS):
+                if 1 <= i <= 6:
+                    at(r + 4, 5, left_form, s + (h,))
+                    at(r + 5, 2, read_left, s + (h,))
+                if i >= 4:
+                    at(r + 4, 5, right_form, s + (h,))
+                    at(r + 5, 2, larger_form, s + (h,))
             pair = c * PAIRS + (i - 5) // 2
-            return pair // 2 if pair % 2 == 1 else None
-
-        def transpose_back(s):
-            k = pass_done_at(s)
-            if k is None:
-                return
-            b = steps[s][0]
-            for h in range(BANKS):
-                for a in range(TILES // 2):
-                    bank = psum.tile([P, 2, 2, P], F32, name="back", tag="back")
-                    for u in range(2):
-                        c, pair = divmod(2 * k + u, PAIRS)
-                        for t in range(2):
-                            words = basis[b, c][:, h, 2 * a + t, 2 * pair : 2 * pair + 2, :]
-                            nc.tensor.transpose(
-                                bank[:, u, t, :], words.rearrange("p j f -> p (j f)").bitcast(F32), ident[:]
-                            )
-                    if a == 0:
-                        grouped[b, h, 1 + k] = planes.tile([P, BANK, PACK], BF16, align_bytes=64, name="grouped", bufs=6)
-                    half_rows = BANK // 2
-                    dst = grouped[b, h, 1 + k][:].rearrange("p n t -> p (n t)").bitcast(F32)
-                    dst = dst[:, a * BANK : (a + 1) * BANK].rearrange("p (n u) -> p n u", u=2)
-                    nc.scalar.copy(out=dst, in_=bank[:].rearrange("p u t n -> p (t n) u"))
-
-        def quantise_at(s):
-            k = pass_done_at(s)
-            if k is not None:
+            if i >= 5 and i % 2 == 1 and pair % 2 == 1:
+                k = pair // 2
                 for h in range(BANKS):
-                    quantise(steps[s][0], h, 1 + k)
-
-        def products_at(s):
-            b, c, i = steps[s]
-            if c < CHUNKS - 1 or i < KNOTS - 1:
-                return
-            for h in range(BANKS):
-                result = rows_pool.tile([P, TILES, UNITS], F32)
-                for a in range(TILES // 2):
-                    acc = psum.tile([P, 2, UNITS], F32, name="acc", tag="misc")
-                    for t in range(2):
-                        cols = slice((2 * a + t) * P, (2 * a + t + 1) * P)
-                        for k in range(PASSES):
-                            nc.tensor.matmul_mx(
-                                out=acc[:, t, :],
-                                lhsT=codes[b, h][:, k, cols].bitcast(FP8X4), lhsT_scale=scales[b, h][:, k, cols],
-                                rhs=w_codes[:, k, :].bitcast(FP8X4), rhs_scale=w_scales[:, k, :],
-                                start=(k == 0), stop=(k == PASSES - 1),
-                            )
-                    nc.vector.tensor_add(out=result[:, 2 * a : 2 * a + 2, :], in0=acc[:], in1=bias[:])
-                nc.sync.dma_start(out=out_banks[b * BANKS + h], in_=result[:])
-
-        def side_jobs(s):
-            b, c, i = steps[s]
-            if 1 <= c <= BANKS and b + 1 < BLOCKS:
+                    for a in range(2):
+                        n = r + 6 + 2 * h + a
+                        at(n, 6, transpose_back, (b, k, h, a))
+                        at(n + 1, 5, regroup, (b, k, h, a))
+                    at(n + 2, 3, quantise, (b, h, 1 + k))
+                    if k == SPLINE_PASSES - 1:
+                        for a in range(2):
+                            at(n + 3 + a, 7, products, (b, h, a))
+                            at(n + 4 + a, 6, add_bias, (b, h, a))
+            if i == 0 and c == CHUNKS - 1:
+                for h in range(BANKS):
+                    at(r + 3 * h, 4, relu_branch, (b, h))
+                    at(r + 3 * h + 2, 5, quantise, (b, h, 0))
+            if i == 0 and 1 <= c <= BANKS and b + 1 < BLOCKS:
                 bank = (b + 1) * BANKS + c - 1
-                if i == 0:
-                    load_rows(bank)
-                if i == 3:
-                    row_statistics(bank)
-                if i == 7:
-                    normalise_and_transpose(bank)
-            if c == CHUNKS - 1 and i < BANKS:
-                relu_branch(b, i)
-            if c == CHUNKS - 1 and 2 <= i < 2 + BANKS:
-                quantise(b, i - 2, 0)
+                at(r, 0, load_rows, (bank,))
+                at(r + 1, 3, row_statistics, (bank,))
+                for t in range(TILES):
+                    at(r + 2 + t // 2, 4, normalise, (bank, t))
+                    at(r + 5 + t, 7, transpose_rows, (bank, t))
+                    at(r + 6 + t, 4, gamma_beta, (bank, t))
 
         for bank in range(BANKS):
             load_rows(bank)
+        roots_of(0)
         with tc.tile_pool(name="wprep", bufs=2) as wprep:
             w_raw = load_weights(wprep)
             for bank in range(BANKS):
                 row_statistics(bank)
+            for c in range(1, CHUNKS):
+                roots_of(c)
+            nc.vector.tensor_mul(out=root_shift[:, 0, :], in0=root[:, 0, :], in1=neg_knots[:, 0, :])
             quantise_weights(wprep, w_raw)
+            nc.vector.tensor_mul(out=root_shift[:, 1:, :], in0=root[:, 1:, :], in1=neg_knots[:, 1:, :])
         pools["work"] = ctx.enter_context(tc.tile_pool(name="work", bufs=2, reuse_waits="tile"))
         for bank in range(BANKS):
-            normalise_and_transpose(bank)
-
-        stages = (square_of, cube_of, terms_of, forms_of, reads_of, transpose_back, quantise_at, products_at)
-        for r in range(len(steps) + len(stages) - 1):
-            if r < len(steps):
-                side_jobs(r)
-            for lag, stage in enumerate(stages):
-                if 0 <= r - lag < len(steps):
-                    stage(r - lag)
+            for t in range(TILES):
+                normalise(bank, t)
+            for c in range(CHUNKS):
+                transpose_rows(bank, c)
+                gamma_beta(bank, c)
+        ctx.enter_context(tc.manual_schedule())
+        for key in sorted(jobs):
+            for job, args in jobs[key]:
+                job(*args)

@@ -19,17 +19,16 @@ UNITS = 256
 KNOTS = 10
 BASES = 6
 CHUNKS = FEATURES // P
-PAIRS = BASES // 2
-HALF_P = P // 2
-SPLINE_PASSES = CHUNKS * PAIRS // 2
-PASSES = 1 + SPLINE_PASSES
-BLOCK = 1024
+OUTER = (0, 1, 4, 5)
+PASSES = 1 + CHUNKS + 2
+PASS_2, PASS_3 = 1 + CHUNKS, 2 + CHUNKS
+BLOCK = 512
 BLOCKS = ROWS // BLOCK
 BANK = 512
 TILES = BANK // P
 BANKS = BLOCK // BANK
 LN_EPS = 0.001
-SCALAR_TERMS = (0, 1, 2)
+SCALAR_TERMS = ((0, 3), (1, 3), (4, 2), (5, 2))
 
 FLOPS = 2 * ROWS * (FEATURES + FEATURES * BASES) * UNITS
 
@@ -60,58 +59,59 @@ def tile_kanlinear_pa_t_kernel(
         bias_bf = const.tile([P, UNITS], BF16)
         nc.scalar.dma_start(out=bias_bf[:], in_=base_bias.partition_broadcast(P))
 
-        gamma = const.tile([P, CHUNKS], F32)
-        beta = const.tile([P, CHUNKS], F32)
-        bias = const.tile([P, 2, UNITS], F32)
         knots = const.tile([P, CHUNKS, KNOTS], F32)
-        nc.vector.tensor_copy(out=gamma[:], in_=gamma_bf[:])
-        nc.vector.tensor_copy(out=beta[:], in_=beta_bf[:])
-        nc.vector.tensor_copy(out=bias[:, 0, :], in_=bias_bf[:])
-        nc.vector.tensor_copy(out=bias[:, 1, :], in_=bias_bf[:])
         nc.vector.tensor_copy(out=knots[:], in_=knots_bf[:])
-        neg_knots = const.tile([P, CHUNKS, KNOTS], F32)
-        nc.vector.tensor_scalar_mul(out=neg_knots[:], in0=knots[:], scalar1=-1.0)
         half = const.tile([P, CHUNKS, KNOTS], F32)
         nc.vector.memset(half[:], 0.5)
         neg_half = const.tile([P, TILES], F32)
         nc.vector.memset(neg_half[:], -0.5)
+        neg_knots = const.tile([P, CHUNKS, KNOTS], F32)
+        nc.vector.tensor_scalar_mul(out=neg_knots[:], in0=knots[:], scalar1=-1.0)
 
         span = {}
         for s in (1, 2, 3, 4):
             span[s] = const.tile([P, CHUNKS, KNOTS - s], F32, name="span%d" % s)
             nc.vector.tensor_sub(out=span[s][:], in0=knots[:, :, s:KNOTS], in1=knots[:, :, 0 : KNOTS - s])
-        inv_span1 = const.tile([P, CHUNKS, KNOTS - 1], F32)
-        nc.vector.reciprocal(out=inv_span1[:], in_=span[1][:])
 
-        ENDS = KNOTS - 3
-        inv_rise = const.tile([P, CHUNKS, ENDS], F32)
-        inv_fall = const.tile([P, CHUNKS, ENDS], F32)
-        rise = const.tile([P, CHUNKS, ENDS], F32)
-        fall = const.tile([P, CHUNKS, ENDS], F32)
-        nc.vector.tensor_mul(out=inv_rise[:], in0=span[1][:, :, 0:ENDS], in1=span[2][:, :, 0:ENDS])
-        nc.vector.tensor_mul(out=inv_rise[:], in0=inv_rise[:], in1=span[3][:])
-        nc.vector.reciprocal(out=rise[:], in_=inv_rise[:])
-        nc.vector.tensor_mul(out=inv_fall[:], in0=span[1][:, :, 2 : 2 + ENDS], in1=span[2][:, :, 1 : 1 + ENDS])
-        nc.vector.tensor_mul(out=inv_fall[:], in0=inv_fall[:], in1=span[3][:])
-        nc.vector.reciprocal(out=fall[:], in_=inv_fall[:])
+        weight = {}
+        for k in range(5):
+            others = [l for l in range(5) if l != k]
+            prod = const.tile([P, CHUNKS, BASES], F32, name="prod%d" % k)
+            gaps = [span[abs(k - l)][:, :, min(k, l) : min(k, l) + BASES] for l in others if abs(k - l) < 4]
+            nc.vector.tensor_mul(out=prod[:], in0=gaps[0], in1=gaps[1])
+            for gap in gaps[2:]:
+                nc.vector.tensor_mul(out=prod[:], in0=prod[:], in1=gap)
+            weight[k] = const.tile([P, CHUNKS, BASES], F32, name="weight%d" % k)
+            nc.vector.reciprocal(out=weight[k][:], in_=prod[:])
+            if 1 <= k <= 3:
+                nc.vector.tensor_mul(out=weight[k][:], in0=weight[k][:], in1=span[4][:])
+            if k % 2 == 1:
+                nc.vector.tensor_scalar_mul(out=weight[k][:], in0=weight[k][:], scalar1=-1.0)
 
-        lead = const.tile([P, CHUNKS, KNOTS], F32)
-        nc.vector.tensor_copy(out=lead[:, :, 0:6], in_=rise[:, :, 0:6])
-        nc.vector.tensor_copy(out=lead[:, :, 6:10], in_=fall[:, :, 3:7])
+        FACTORS = {2: (0, 2, 1), 3: (1, 2, -1), 4: (4, 0, 1), 5: (4, 1, 1), 6: (3, 3, -1), 7: (4, 3, 1)}
+        factor = const.tile([P, CHUNKS, KNOTS], F32)
+        nc.vector.memset(factor[:], 1.0)
+        for i in FACTORS:
+            k, j, sign = FACTORS[i]
+            nc.vector.tensor_scalar_mul(
+                out=factor[:, :, i : i + 1], in0=weight[k][:, :, j : j + 1], scalar1=float(sign)
+            )
+        inv_factor = const.tile([P, CHUNKS, KNOTS], F32)
+        nc.vector.reciprocal(out=inv_factor[:], in_=factor[:])
         root = const.tile([P, CHUNKS, KNOTS], F32)
         root_shift = const.tile([P, CHUNKS, KNOTS], F32)
-        swap = const.tile([P, CHUNKS, 3], F32)
-        nc.vector.tensor_mul(out=swap[:], in0=inv_rise[:, :, 3:6], in1=fall[:, :, 0:3])
-        swap_back = const.tile([P, CHUNKS, 1], F32)
-        nc.vector.tensor_mul(out=swap_back[:], in0=inv_fall[:, :, 3:4], in1=rise[:, :, 6:7])
-        left_second = const.tile([P, CHUNKS, BASES], F32)
-        right_second = const.tile([P, CHUNKS, BASES], F32)
-        nc.vector.tensor_mul(out=left_second[:], in0=span[4][:], in1=inv_span1[:, :, 0:BASES])
-        nc.vector.tensor_scalar_mul(out=left_second[:], in0=left_second[:], scalar1=-1.0)
-        nc.vector.tensor_mul(out=left_second[:, :, 5:6], in0=left_second[:, :, 5:6], in1=swap_back[:])
-        nc.vector.tensor_mul(out=right_second[:], in0=span[4][:], in1=inv_span1[:, :, 3 : 3 + BASES])
-        nc.vector.tensor_scalar_mul(out=right_second[:], in0=right_second[:], scalar1=-1.0)
-        nc.vector.tensor_mul(out=right_second[:, :, 0:3], in0=right_second[:, :, 0:3], in1=swap[:])
+        coef = {}
+        for k in range(5):
+            coef[k] = const.tile([P, CHUNKS, BASES], F32, name="coef%d" % k)
+            nc.vector.tensor_mul(out=coef[k][:], in0=weight[k][:], in1=inv_factor[:, :, k : k + BASES])
+
+        gamma = const.tile([P, CHUNKS], F32)
+        beta = const.tile([P, CHUNKS], F32)
+        bias = const.tile([P, 2, UNITS], F32)
+        nc.vector.tensor_copy(out=gamma[:], in_=gamma_bf[:])
+        nc.vector.tensor_copy(out=beta[:], in_=beta_bf[:])
+        nc.vector.tensor_copy(out=bias[:, 0, :], in_=bias_bf[:])
+        nc.vector.tensor_copy(out=bias[:, 1, :], in_=bias_bf[:])
 
         w_codes = const.tile([P, PASSES, UNITS], U32, align_bytes=64)
         w_scales = const.tile([P, PASSES, UNITS], U8, align_bytes=64)
@@ -119,15 +119,18 @@ def tile_kanlinear_pa_t_kernel(
         def load_weights(pool):
             w_raw = pool.tile([P, PASSES * PACK, UNITS], BF16, bufs=1)
             nc.scalar.dma_start(out=w_raw[:, 0:PACK, :], in_=base_weight.rearrange("(t p) u -> p t u", p=P))
-            by_plane = spline_weight.rearrange("(c m e k o) u -> c o e m k u", c=CHUNKS, e=2, k=PAIRS, o=2)
+            by_pair = spline_weight.rearrange("(c m e k) u -> c e m k u", c=CHUNKS, e=2, k=BASES)
             for c in range(CHUNKS):
                 for o in range(2):
                     for e in range(2):
-                        first = PACK + 2 * PAIRS * c + e
+                        first = PACK * (1 + c) + e
                         nc.scalar.dma_start(
-                            out=w_raw[o * HALF_P : (o + 1) * HALF_P, first : first + 2 * PAIRS - 1 : 2, :],
-                            in_=by_plane[c, o, e],
+                            out=w_raw[o * P // 2 : (o + 1) * P // 2, first : first + 3 : 2, :],
+                            in_=by_pair[c, e, :, o : o + 5 : 4, :],
                         )
+            by_basis = spline_weight.rearrange("(c p k) u -> k p c u", p=P, k=BASES)
+            for k, j in ((PASS_2, 2), (PASS_3, 3)):
+                nc.scalar.dma_start(out=w_raw[:, PACK * k : PACK * (k + 1), :], in_=by_basis[j])
             return w_raw
 
         def quantise_weights(pool, w_raw):
@@ -143,16 +146,16 @@ def tile_kanlinear_pa_t_kernel(
                 )
 
         x_banks = x.rearrange("(b t p) f -> b p t f", t=TILES, p=P)
-        out_banks = out.rearrange("(b t p) u -> b p t u", t=TILES, p=P)
+        out_pairs = out.rearrange("(b t p) u -> b p t u", t=2, p=P)
 
         x_sb, row_scale, row_shift, z, z_t, xn = {}, {}, {}, {}, {}, {}
-        square, cube, left_term, right_term, right_lead = {}, {}, {}, {}, {}
-        left, right, left_bf, basis, back, grouped = {}, {}, {}, {}, {}, {}
-        codes, scales, acc, result = {}, {}, {}, {}
+        square, cube, term, inner_term, form = {}, {}, {}, {}, {}
+        bank_sum, basis, inner, back, grouped = {}, {}, {}, {}, {}
+        codes, scales, acc = {}, {}, {}
         pools, jobs = {}, {}
 
         def roots_of(c):
-            nc.gpsimd.tensor_tensor(out=root[:, c, :], in0=lead[:, c, :], in1=half[:, c, :], op=ALU.pow)
+            nc.gpsimd.tensor_tensor(out=root[:, c, :], in0=factor[:, c, :], in1=half[:, c, :], op=ALU.pow)
 
         def load_rows(bank):
             x_sb[bank] = rows_pool.tile([P, TILES, FEATURES], BF16, name="x_sb")
@@ -198,10 +201,13 @@ def tile_kanlinear_pa_t_kernel(
                 scale=gamma[:, c : c + 1], bias=beta[:, c : c + 1],
             )
 
+        def new_group(b, h, k):
+            grouped[b, h, k] = planes.tile([P, BANK, PACK], BF16, align_bytes=64, name="grouped", bufs=6)
+            return grouped[b, h, k]
+
         def relu_branch(b, h):
-            grouped[b, h, 0] = planes.tile([P, BANK, PACK], BF16, align_bytes=64, name="grouped", bufs=6)
             nc.scalar.activation(
-                out=grouped[b, h, 0][:],
+                out=new_group(b, h, 0)[:],
                 in_=xn[b][:, :, h * BANK : (h + 1) * BANK].rearrange("p t n -> p n t"), func=ACT.Relu,
             )
 
@@ -222,98 +228,102 @@ def tile_kanlinear_pa_t_kernel(
             )
 
         def cube_of(b, c, i):
-            cube[b, c, i] = pools["work"].tile([P, BLOCK], F32, name="cube", bufs=6)
+            cube[b, c, i] = pools["work"].tile([P, BLOCK], F32, name="cube", bufs=10)
             nc.vector.scalar_tensor_tensor(
                 out=cube[b, c, i][:], in0=xn[b][:, c, :], scalar=knots[:, c, i : i + 1], in1=square[b, c, i][:],
                 op0=ALU.subtract, op1=ALU.mult,
             )
 
-        def terms_of(b, c, i):
-            s = (b, c, i)
-            if 1 <= i <= 6:
-                j = i - 1
-                left_term[s] = pools["work"].tile([P, BLOCK], F32, name="left_term", bufs=2)
+        def term_of(b, c, i, j):
+            k = i - j
+            term[b, c, j, k] = pools["work"].tile([P, BLOCK], F32, name="term", bufs=20)
+            dst, src, scale = term[b, c, j, k][:], cube[b, c, i][:], coef[k][:, c, j : j + 1]
+            if k == 0:
+                nc.vector.tensor_scalar_mul(out=dst, in0=src, scalar1=scale)
+            elif (j, k) in SCALAR_TERMS:
+                nc.scalar.activation(out=dst, in_=src, func=ACT.Relu, scale=scale)
+            else:
                 nc.vector.tensor_scalar(
-                    out=left_term[s][:], in0=cube[s][:], scalar1=0.0, scalar2=left_second[:, c, j : j + 1],
-                    op0=ALU.max, op1=ALU.mult,
-                )
-            if 3 <= i <= 8:
-                j = i - 3
-                right_term[s] = pools["work"].tile([P, BLOCK], F32, name="right_term", bufs=4)
-                if j in SCALAR_TERMS:
-                    nc.scalar.activation(
-                        out=right_term[s][:], in_=cube[s][:], func=ACT.Relu, scale=right_second[:, c, j : j + 1]
-                    )
-                else:
-                    nc.vector.tensor_scalar(
-                        out=right_term[s][:], in0=cube[s][:], scalar1=0.0, scalar2=right_second[:, c, j : j + 1],
-                        op0=ALU.min, op1=ALU.mult,
-                    )
-            if 4 <= i <= 5:
-                right_lead[s] = pools["work"].tile([P, BLOCK], F32, name="right_lead", bufs=2)
-                nc.vector.tensor_scalar_mul(
-                    out=right_lead[s][:], in0=cube[s][:], scalar1=swap[:, c, i - 3 : i - 2]
+                    out=dst, in0=src, scalar1=0.0, scalar2=scale, op0=ALU.min if j < 2 else ALU.max, op1=ALU.mult
                 )
 
-        def add_up(bank, first, second, h):
+        def add_up(b, c, j, h):
+            bank_sum[b, c, j, h] = psum.tile([P, BANK], F32, name="bank_sum", tag="sum", bufs=4)
+            if j < 2:
+                parts = [cube[b, c, j + 4]] + [term[b, c, j, k] for k in (3, 2, 1)]
+            else:
+                parts = [term[b, c, j, k] for k in (0, 1, 2, 3)]
             for t in range(TILES):
                 rows = slice(h * BANK + t * P, h * BANK + (t + 1) * P)
-                for term, start in ((first, True), (second, False)):
+                for n, part in enumerate(parts):
                     nc.tensor.matmul(
-                        bank[:, t * P : (t + 1) * P], lhsT=term[:, rows], rhs=ident[:],
-                        is_transpose=True, start=start, stop=not start,
+                        bank_sum[b, c, j, h][:, t * P : (t + 1) * P], lhsT=part[:, rows], rhs=ident[:],
+                        is_transpose=True, start=(n == 0), stop=(n == 3),
                     )
 
-        def keep_clock(bank):
-            nc.tensor.matmul_mx(
-                out=bank[:],
-                lhsT=w_codes[:, 0, 0:P].bitcast(FP8X4), lhsT_scale=w_scales[:, 0, 0:P],
-                rhs=w_codes[:, 0:2, :].rearrange("p k u -> p (k u)").bitcast(FP8X4),
-                rhs_scale=w_scales[:, 0:2, :].rearrange("p k u -> p (k u)"),
-                start=True, stop=True,
+        def read_sum(b, c, j, h):
+            if j == OUTER[0] and h == 0:
+                basis[b, c] = planes.tile([P, BANKS, TILES, len(OUTER), P], BF16, name="basis")
+            nc.scalar.activation(
+                out=basis[b, c][:, h, :, OUTER.index(j), :],
+                in_=bank_sum[b, c, j, h][:].rearrange("p (t f) -> p t f", f=P),
+                func=ACT.Relu, scale=-1.0 if j < 2 else 1.0,
             )
 
-        def left_form(b, c, i, h):
-            left[b, c, i, h] = psum.tile([P, BANK], F32, name="left", tag="left")
-            keep_clock(left[b, c, i, h])
-            add_up(left[b, c, i, h], cube[b, c, i - 1], left_term[b, c, i], h)
-
-        def right_form(b, c, i, h):
-            right[b, c, i, h] = psum.tile([P, BANK], F32, name="right", tag="right")
-            first = right_lead[b, c, i] if i <= 5 else cube[b, c, i]
-            add_up(right[b, c, i, h], first, right_term[b, c, i - 1], h)
-
-        def read_left(b, c, i, h):
-            j = i - 1
-            left_bf[b, c, j, h] = planes.tile([P, BANK], BF16, name="left_bf", bufs=12)
-            nc.scalar.activation(out=left_bf[b, c, j, h][:], in_=left[b, c, i, h][:], func=ACT.Relu)
-
-        def larger_form(b, c, i, h):
-            j = i - 4
-            if j == 0 and h == 0:
-                basis[b, c] = planes.tile([P, BANKS, TILES, BASES, P], BF16, name="basis")
-            nc.vector.scalar_tensor_tensor(
-                out=basis[b, c][:, h, :, j, :], in0=right[b, c, i, h][:].rearrange("p (t f) -> p t f", f=P),
-                scalar=-1.0, in1=left_bf[b, c, j, h][:].rearrange("p (t f) -> p t f", f=P),
-                op0=ALU.mult, op1=ALU.max,
-            )
-
-        def transpose_back(b, k, h, a):
-            back[b, k, h, a] = psum.tile([P, 2, 2, P], F32, name="back", tag="back")
+        def transpose_back(b, c, h, a):
+            back[b, c, h, a] = psum.tile([P, 2, 2, P], F32, name="back", tag="back")
             for u in range(2):
-                c, pair = divmod(2 * k + u, PAIRS)
                 for t in range(2):
-                    words = basis[b, c][:, h, 2 * a + t, 2 * pair : 2 * pair + 2, :]
+                    words = basis[b, c][:, h, 2 * a + t, 2 * u : 2 * u + 2, :]
                     nc.tensor.transpose(
-                        back[b, k, h, a][:, u, t, :], words.rearrange("p j f -> p (j f)").bitcast(F32), ident[:]
+                        back[b, c, h, a][:, u, t, :], words.rearrange("p j f -> p (j f)").bitcast(F32), ident[:]
                     )
 
-        def regroup(b, k, h, a):
+        def regroup(b, c, h, a):
             if a == 0:
-                grouped[b, h, 1 + k] = planes.tile([P, BANK, PACK], BF16, align_bytes=64, name="grouped", bufs=6)
-            dst = grouped[b, h, 1 + k][:].rearrange("p n t -> p (n t)").bitcast(F32)
+                new_group(b, h, 1 + c)
+            dst = grouped[b, h, 1 + c][:].rearrange("p n t -> p (n t)").bitcast(F32)
             dst = dst[:, a * BANK : (a + 1) * BANK].rearrange("p (n u) -> p n u", u=2)
-            nc.scalar.copy(out=dst, in_=back[b, k, h, a][:].rearrange("p u t n -> p (t n) u"))
+            nc.scalar.copy(out=dst, in_=back[b, c, h, a][:].rearrange("p u t n -> p (t n) u"))
+
+        def inner_term_of(b, c, i):
+            inner_term[b, c, i] = pools["work"].tile([P, BLOCK], F32, name="inner_term", bufs=2)
+            j, k = (3, 1) if i == 4 else (2, 3)
+            nc.vector.tensor_scalar(
+                out=inner_term[b, c, i][:], in0=cube[b, c, i][:], scalar1=0.0, scalar2=coef[k][:, c, j : j + 1],
+                op0=ALU.max if i == 4 else ALU.min, op1=ALU.mult,
+            )
+
+        def form_of(b, c, i):
+            form[b, c, i] = planes.tile([P, BLOCK], BF16, name="form", bufs=6)
+            dst = form[b, c, i][:]
+            if i == 3:
+                nc.vector.scalar_tensor_tensor(
+                    out=dst, in0=cube[b, c, 3][:], scalar=0.0, in1=cube[b, c, 2][:], op0=ALU.max, op1=ALU.subtract
+                )
+            elif i == 7:
+                nc.vector.scalar_tensor_tensor(
+                    out=dst, in0=cube[b, c, 6][:], scalar=0.0, in1=cube[b, c, 7][:], op0=ALU.min, op1=ALU.subtract
+                )
+            else:
+                source, j, k = (3, 3, 0) if i == 4 else (6, 2, 4)
+                nc.vector.scalar_tensor_tensor(
+                    out=dst, in0=cube[b, c, source][:], scalar=coef[k][:, c, j : j + 1],
+                    in1=inner_term[b, c, i if i == 4 else 5][:], op0=ALU.mult, op1=ALU.add,
+                )
+
+        def inner_basis(b, c, j):
+            if c == 0:
+                inner[b, j] = planes.tile([P, CHUNKS, BLOCK], BF16, name="inner%d" % j, bufs=1)
+            nc.vector.tensor_tensor(
+                out=inner[b, j][:, c, :], in0=form[b, c, 3 if j == 2 else 4][:], in1=form[b, c, 6 if j == 2 else 7][:],
+                op=ALU.min if j == 2 else ALU.max,
+            )
+
+        def regroup_inner(b, j, h):
+            dst = new_group(b, h, PASS_2 if j == 2 else PASS_3)[:].rearrange("p (a i) t -> p a t i", i=4)
+            src = inner[b, j][:, :, h * BANK : (h + 1) * BANK].rearrange("p t (a i) -> p a t i", i=4)
+            nc.scalar.activation(out=dst, in_=src, func=ACT.Relu, scale=-1.0 if j == 2 else 1.0)
 
         def products(b, h, a):
             acc[b, h, a] = psum.tile([P, 2, UNITS], F32, name="acc", tag="misc")
@@ -328,62 +338,64 @@ def tile_kanlinear_pa_t_kernel(
                     )
 
         def add_bias(b, h, a):
-            if a == 0:
-                result[b, h] = rows_pool.tile([P, TILES, UNITS], F32, name="result")
-            nc.vector.tensor_add(out=result[b, h][:, 2 * a : 2 * a + 2, :], in0=acc[b, h, a][:], in1=bias[:])
-            if a == TILES // 2 - 1:
-                nc.sync.dma_start(out=out_banks[b * BANKS + h], in_=result[b, h][:])
+            result = rows_pool.tile([P, 2, UNITS], F32)
+            nc.vector.tensor_add(out=result[:], in0=acc[b, h, a][:], in1=bias[:])
+            nc.sync.dma_start(out=out_pairs[(b * BANKS + h) * 2 + a], in_=result[:])
 
-        HALF = KNOTS // 2
         chunks = [(b, c) for b in range(BLOCKS) for c in range(CHUNKS)]
-        steps = []
-        for m in range(len(chunks) + 1):
-            for i in range(HALF):
-                if m < len(chunks):
-                    steps.append(chunks[m] + (i,))
-                if m > 0:
-                    steps.append(chunks[m - 1] + (i + HALF,))
+        steps = [chunk + (i,) for chunk in chunks for i in range(1, KNOTS - 1)]
+        TERMS = {
+            1: (0,), 2: (0, 1), 3: (0, 1), 4: (1, 4), 5: (4, 5), 6: (4, 5), 7: (4, 5), 8: (5,),
+        }
+        DONE = {4: 0, 5: 1, 7: 4, 8: 5}
 
         def at(r, rank, job, args):
             jobs.setdefault((r, rank), []).append((job, args))
 
         for r, s in enumerate(steps):
             b, c, i = s
-            at(r, 3, square_of, s)
-            at(r + 2, 1, cube_of, s)
-            at(r + 3, 2, terms_of, s)
-            for h in range(BANKS):
-                if 1 <= i <= 6:
-                    at(r + 4, 5, left_form, s + (h,))
-                    at(r + 5, 2, read_left, s + (h,))
-                if i >= 4:
-                    at(r + 4, 5, right_form, s + (h,))
-                    at(r + 5, 2, larger_form, s + (h,))
-            pair = c * PAIRS + (i - 5) // 2
-            if i >= 5 and i % 2 == 1 and pair % 2 == 1:
-                k = pair // 2
+            at(r, 2, square_of, s)
+            at(r + 2, 2, cube_of, s)
+            for j in TERMS[i]:
+                at(r + 3, 3, term_of, s + (j,))
+            if i == 4 or i == 5:
+                at(r + 3, 3, inner_term_of, s)
+            if i in (3, 4, 6, 7):
+                at(r + 4, 1, form_of, s)
+            if i in (6, 7):
+                at(r + 5, 1, inner_basis, (b, c, 2 if i == 6 else 3))
+            if i in DONE:
+                j = DONE[i]
                 for h in range(BANKS):
-                    for a in range(2):
-                        n = r + 6 + 2 * h + a
-                        at(n, 6, transpose_back, (b, k, h, a))
-                        at(n + 1, 5, regroup, (b, k, h, a))
-                    at(n + 2, 3, quantise, (b, h, 1 + k))
-                    if k == SPLINE_PASSES - 1:
+                    n = r + (5, 6, 6, 7)[OUTER.index(j)] + h
+                    at(n, 5, add_up, (b, c, j, h))
+                    at(n + 2, 1, read_sum, (b, c, j, h))
+                    if j == OUTER[-1]:
                         for a in range(2):
-                            at(n + 3 + a, 7, products, (b, h, a))
-                            at(n + 4 + a, 6, add_bias, (b, h, a))
-            if i == 0 and c == CHUNKS - 1:
+                            at(n + 2 + 1 + a, 6, transpose_back, (b, c, h, a))
+                            at(n + 2 + 2 + a, 3, regroup, (b, c, h, a))
+                        at(n + 2 + 4, 3, quantise, (b, h, 1 + c))
+                        if c == CHUNKS - 1:
+                            for a in range(2):
+                                at(n + 2 + 5 + a, 7, products, (b, h, a))
+                                at(n + 2 + 6 + a, 6, add_bias, (b, h, a))
+            if c == CHUNKS - 1 and i in (6, 7):
+                j = 2 if i == 6 else 3
                 for h in range(BANKS):
-                    at(r + 3 * h, 4, relu_branch, (b, h))
-                    at(r + 3 * h + 2, 5, quantise, (b, h, 0))
-            if i == 0 and 1 <= c <= BANKS and b + 1 < BLOCKS:
-                bank = (b + 1) * BANKS + c - 1
+                    at(r + 5 + 1 + h, 3, regroup_inner, (b, j, h))
+                    at(r + 10 + h, 3, quantise, (b, h, PASS_2 if j == 2 else PASS_3))
+            if c == 2 and i == 1:
+                for h in range(BANKS):
+                    at(r + 2 * h, 4, relu_branch, (b, h))
+                    at(r + 2 * h + 3, 3, quantise, (b, h, 0))
+            if i == 1 and c == 0 and b + 1 < BLOCKS:
+                bank = b + 1
                 at(r, 0, load_rows, (bank,))
-                at(r + 1, 3, row_statistics, (bank,))
+                at(r + 6, 3, row_statistics, (bank,))
                 for t in range(TILES):
-                    at(r + 2 + t // 2, 4, normalise, (bank, t))
-                    at(r + 5 + t, 7, transpose_rows, (bank, t))
-                    at(r + 6 + t, 4, gamma_beta, (bank, t))
+                    at(r + 10 + t, 4, normalise, (bank, t))
+                    at(r + 15 + 2 * t, 7, transpose_rows, (bank, t))
+                    at(r + 15 + 2 * t + 1, 4, gamma_beta, (bank, t))
 
         for bank in range(BANKS):
             load_rows(bank)

@@ -44,6 +44,7 @@ def tile_kanlinear_pa_t_kernel(
         xn_pool = ctx.enter_context(tc.tile_pool(name="xn", bufs=2))
         planes = ctx.enter_context(tc.tile_pool(name="planes", bufs=2))
         mx = ctx.enter_context(tc.tile_pool(name="mx", bufs=2))
+        work = ctx.enter_context(tc.tile_pool(name="work", bufs=2))
         psum = ctx.enter_context(tc.psum_pool(name="psum", bufs=2))
 
         ident = const.tile([P, P], F32)
@@ -67,6 +68,314 @@ def tile_kanlinear_pa_t_kernel(
         nc.vector.memset(neg_half[:], -0.5)
         neg_knots = const.tile([P, CHUNKS, KNOTS], F32)
         nc.vector.tensor_scalar_mul(out=neg_knots[:], in0=knots[:], scalar1=-1.0)
+
+        w_codes = const.tile([P, PASSES, UNITS], U32, align_bytes=64)
+        w_scales = const.tile([P, PASSES, UNITS], U8, align_bytes=64)
+
+        def load_weights():
+            w_raw = const.tile([P, PASSES * PACK, UNITS], BF16)
+            nc.sync.dma_start(out=w_raw[:, 0:PACK, :], in_=base_weight.rearrange("(t p) u -> p t u", p=P))
+            by_pair = spline_weight.rearrange("(c m e k) u -> c e m k u", c=CHUNKS, e=2, k=BASES)
+            for c in range(CHUNKS):
+                for o in range(2):
+                    for e in range(2):
+                        first = PACK * (1 + c) + e
+                        nc.sync.dma_start(
+                            out=w_raw[o * P // 2 : (o + 1) * P // 2, first : first + 3 : 2, :],
+                            in_=by_pair[c, e, :, o : o + 5 : 4, :],
+                        )
+            by_basis = spline_weight.rearrange("(c p k) u -> k p c u", p=P, k=BASES)
+            for k, j in ((PASS_2, 2), (PASS_3, 3)):
+                nc.sync.dma_start(out=w_raw[:, PACK * k : PACK * (k + 1), :], in_=by_basis[j])
+            return w_raw
+
+        def group_weights(k):
+            w_grouped[k] = small.tile([P, UNITS, PACK], BF16, name="w_grouped", align_bytes=64)
+            nc.vector.tensor_copy(
+                out=w_grouped[k][:], in_=w_raw[:, k * PACK : (k + 1) * PACK, :].rearrange("p t u -> p u t")
+            )
+
+        def quantise_weights(k):
+            nc.vector.quantize_mx(
+                out=w_codes[:, k, :].bitcast(FP8X4),
+                scales=w_scales[:, k, :],
+                in_=w_grouped[k][:].rearrange("p u t -> p (u t)"),
+            )
+
+        x_banks = x.rearrange("(b t p) f -> b p t f", t=TILES, p=P)
+        out_pairs = out.rearrange("(b t p) u -> b p t u", t=2, p=P)
+
+        x_sb, row_scale, row_shift, z, z_t, xn = {}, {}, {}, {}, {}, {}
+        square, cube, term, inner_term, form = {}, {}, {}, {}, {}
+        bank_sum, basis, inner, back, grouped = {}, {}, {}, {}, {}
+        codes, scales, acc, w_grouped = {}, {}, {}, {}
+        jobs = {}
+
+        def roots_of(c):
+            nc.gpsimd.tensor_tensor(out=root[:, c, :], in0=factor[:, c, :], in1=half[:, c, :], op=ALU.pow)
+
+        def load_rows(bank, tiles):
+            if bank not in x_sb:
+                x_sb[bank] = rows_pool.tile([P, TILES, FEATURES], BF16, name="x_sb")
+            nc.sync.dma_start(out=x_sb[bank][:, tiles, :], in_=x_banks[bank][:, tiles, :])
+
+        def row_statistics(bank, tiles):
+            if bank not in row_scale:
+                row_scale[bank] = small.tile([P, TILES], F32, name="row_scale")
+                row_shift[bank] = small.tile([P, TILES], F32, name="row_shift")
+            stats = small.tile([P, TILES, 6], F32)
+            mean_var = small.tile([P, TILES, 2], F32)
+            for t in range(tiles.start, tiles.stop):
+                nc.vector.bn_stats(out=stats[:, t, :], in_=x_sb[bank][:, t, :])
+            for t in range(tiles.start, tiles.stop):
+                nc.vector.bn_aggr(out=mean_var[:, t, :], in_=stats[:, t, :])
+            var_eps = small.tile([P, TILES], F32)
+            nc.vector.tensor_scalar_add(out=var_eps[:, tiles], in0=mean_var[:, tiles, 1], scalar1=LN_EPS)
+            neg_mean = small.tile([P, TILES], F32)
+            nc.vector.tensor_scalar_mul(out=neg_mean[:, tiles], in0=mean_var[:, tiles, 0], scalar1=-1.0)
+            nc.gpsimd.tensor_tensor(
+                out=row_scale[bank][:, tiles], in0=var_eps[:, tiles], in1=neg_half[:, tiles], op=ALU.pow
+            )
+            nc.gpsimd.tensor_tensor(
+                out=row_shift[bank][:, tiles], in0=neg_mean[:, tiles], in1=row_scale[bank][:, tiles], op=ALU.mult
+            )
+
+        def normalise(bank, t):
+            if t == 0:
+                z[bank] = rows_pool.tile([P, TILES, FEATURES], F32, name="z", bufs=1)
+            nc.scalar.activation(
+                out=z[bank][:, t, :], in_=x_sb[bank][:, t, :], func=ACT.Identity,
+                scale=row_scale[bank][:, t : t + 1], bias=row_shift[bank][:, t : t + 1],
+            )
+
+        def transpose_rows(bank, c):
+            z_t[bank, c] = psum.tile([P, BANK], F32, name="z_t", tag="back")
+            for t in range(TILES):
+                nc.tensor.transpose(
+                    z_t[bank, c][:, t * P : (t + 1) * P], z[bank][:, t, c * P : (c + 1) * P], ident[:]
+                )
+
+        def gamma_beta(bank, c):
+            b, h = divmod(bank, BANKS)
+            if h == 0 and c == 0:
+                xn[b] = xn_pool.tile([P, CHUNKS, BLOCK], F32, name="xn")
+            nc.scalar.activation(
+                out=xn[b][:, c, h * BANK : (h + 1) * BANK], in_=z_t[bank, c][:], func=ACT.Identity,
+                scale=gamma[:, c : c + 1], bias=beta[:, c : c + 1],
+            )
+
+        def new_group(b, h, k):
+            grouped[b, h, k] = planes.tile([P, BANK, PACK], BF16, align_bytes=64, name="grouped", bufs=7)
+            return grouped[b, h, k]
+
+        def relu_branch(b, h):
+            nc.scalar.activation(
+                out=new_group(b, h, 0)[:],
+                in_=xn[b][:, :, h * BANK : (h + 1) * BANK].rearrange("p t n -> p n t"), func=ACT.Relu,
+            )
+
+        def quantise(b, h, k):
+            if (b, h) not in codes:
+                codes[b, h] = mx.tile([P, PASSES, BANK], U32, align_bytes=64, name="codes")
+                scales[b, h] = mx.tile([P, PASSES, BANK], U8, align_bytes=64, name="scales")
+            nc.vector.quantize_mx(
+                out=codes[b, h][:, k, :].bitcast(FP8X4), scales=scales[b, h][:, k, :],
+                in_=grouped[b, h, k][:].rearrange("p n t -> p (n t)"),
+            )
+
+        def square_of(b, c, i):
+            square[b, c, i] = work.tile([P, BLOCK], F32, name="square", bufs=4)
+            nc.scalar.activation(
+                out=square[b, c, i][:], in_=xn[b][:, c, :], func=ACT.Square,
+                scale=root[:, c, i : i + 1], bias=root_shift[:, c, i : i + 1],
+            )
+
+        def cube_of(b, c, i):
+            cube[b, c, i] = work.tile([P, BLOCK], F32, name="cube", bufs=10)
+            nc.vector.scalar_tensor_tensor(
+                out=cube[b, c, i][:], in0=xn[b][:, c, :], scalar=knots[:, c, i : i + 1], in1=square[b, c, i][:],
+                op0=ALU.subtract, op1=ALU.mult,
+            )
+
+        def term_of(b, c, i, j):
+            k = i - j
+            term[b, c, j, k] = work.tile([P, BLOCK], F32, name="term", bufs=22)
+            dst, src, scale = term[b, c, j, k][:], cube[b, c, i][:], coef[k][:, c, j : j + 1]
+            if k == 0:
+                nc.vector.tensor_scalar_mul(out=dst, in0=src, scalar1=scale)
+            elif (j, k) in SCALAR_TERMS:
+                nc.scalar.activation(out=dst, in_=src, func=ACT.Relu, scale=scale)
+            else:
+                nc.vector.tensor_scalar(
+                    out=dst, in0=src, scalar1=0.0, scalar2=scale, op0=ALU.min if j < 2 else ALU.max, op1=ALU.mult
+                )
+
+        def add_up(b, c, pair, h):
+            parts = {}
+            for j in pair:
+                bank_sum[b, c, j, h] = psum.tile([P, BANK], F32, name="bank_sum", tag="sum", bufs=4)
+                if j < 2:
+                    parts[j] = [cube[b, c, j + 4]] + [term[b, c, j, k] for k in (3, 2, 1)]
+                else:
+                    parts[j] = [term[b, c, j, k] for k in (0, 1, 2, 3)]
+            for t in range(TILES):
+                rows = slice(h * BANK + t * P, h * BANK + (t + 1) * P)
+                for n in range(4):
+                    for j in pair:
+                        nc.tensor.matmul(
+                            bank_sum[b, c, j, h][:, t * P : (t + 1) * P], lhsT=parts[j][n][:, rows], rhs=ident[:],
+                            is_transpose=True, start=(n == 0), stop=(n == 3),
+                        )
+
+        def read_sum(b, c, j, h):
+            if j == OUTER[0] and h == 0:
+                basis[b, c] = planes.tile([P, BANKS, TILES, len(OUTER), P], BF16, name="basis")
+            nc.scalar.activation(
+                out=basis[b, c][:, h, :, OUTER.index(j), :],
+                in_=bank_sum[b, c, j, h][:].rearrange("p (t f) -> p t f", f=P),
+                func=ACT.Relu, scale=-1.0 if j < 2 else 1.0,
+            )
+
+        def transpose_back(b, c, h, a):
+            back[b, c, h, a] = psum.tile([P, 2, 2, P], F32, name="back", tag="back")
+            for u in range(2):
+                for t in range(2):
+                    words = basis[b, c][:, h, 2 * a + t, 2 * u : 2 * u + 2, :]
+                    nc.tensor.transpose(
+                        back[b, c, h, a][:, u, t, :], words.rearrange("p j f -> p (j f)").bitcast(F32), ident[:]
+                    )
+
+        def regroup(b, c, h, a):
+            if a == 0:
+                new_group(b, h, 1 + c)
+            dst = grouped[b, h, 1 + c][:].rearrange("p n t -> p (n t)").bitcast(F32)
+            dst = dst[:, a * BANK : (a + 1) * BANK].rearrange("p (n u) -> p n u", u=2)
+            nc.scalar.copy(out=dst, in_=back[b, c, h, a][:].rearrange("p u t n -> p (t n) u"))
+
+        def inner_term_of(b, c, i):
+            inner_term[b, c, i] = work.tile([P, BLOCK], F32, name="inner_term", bufs=2)
+            j, k = (3, 1) if i == 4 else (2, 3)
+            nc.vector.tensor_scalar(
+                out=inner_term[b, c, i][:], in0=cube[b, c, i][:], scalar1=0.0, scalar2=coef[k][:, c, j : j + 1],
+                op0=ALU.max if i == 4 else ALU.min, op1=ALU.mult,
+            )
+
+        def form_of(b, c, i):
+            form[b, c, i] = planes.tile([P, BLOCK], BF16, name="form", bufs=6)
+            dst = form[b, c, i][:]
+            if i == 3:
+                nc.vector.scalar_tensor_tensor(
+                    out=dst, in0=cube[b, c, 3][:], scalar=0.0, in1=cube[b, c, 2][:], op0=ALU.max, op1=ALU.subtract
+                )
+            elif i == 7:
+                nc.vector.scalar_tensor_tensor(
+                    out=dst, in0=cube[b, c, 6][:], scalar=0.0, in1=cube[b, c, 7][:], op0=ALU.min, op1=ALU.subtract
+                )
+            else:
+                source, j, k = (3, 3, 0) if i == 4 else (6, 2, 4)
+                nc.vector.scalar_tensor_tensor(
+                    out=dst, in0=cube[b, c, source][:], scalar=coef[k][:, c, j : j + 1],
+                    in1=inner_term[b, c, i if i == 4 else 5][:], op0=ALU.mult, op1=ALU.add,
+                )
+
+        def inner_basis(b, c, j):
+            if c == 0:
+                inner[b, j] = planes.tile([P, CHUNKS, BLOCK], BF16, name="inner%d" % j, bufs=1)
+            nc.vector.tensor_tensor(
+                out=inner[b, j][:, c, :], in0=form[b, c, 3 if j == 2 else 4][:], in1=form[b, c, 6 if j == 2 else 7][:],
+                op=ALU.min if j == 2 else ALU.max,
+            )
+
+        def regroup_inner(b, j, h):
+            dst = new_group(b, h, PASS_2 if j == 2 else PASS_3)[:].rearrange("p (a i) t -> p a t i", i=4)
+            src = inner[b, j][:, :, h * BANK : (h + 1) * BANK].rearrange("p t (a i) -> p a t i", i=4)
+            nc.scalar.activation(out=dst, in_=src, func=ACT.Relu, scale=-1.0 if j == 2 else 1.0)
+
+        def products(b, h, a):
+            acc[b, h, a] = psum.tile([P, 2, UNITS], F32, name="acc", tag="acc")
+            for t in range(2):
+                cols = slice((2 * a + t) * P, (2 * a + t + 1) * P)
+                for k in range(PASSES):
+                    nc.tensor.matmul_mx(
+                        out=acc[b, h, a][:, t, :],
+                        lhsT=codes[b, h][:, k, cols].bitcast(FP8X4), lhsT_scale=scales[b, h][:, k, cols],
+                        rhs=w_codes[:, k, :].bitcast(FP8X4), rhs_scale=w_scales[:, k, :],
+                        start=(k == 0), stop=(k == PASSES - 1),
+                    )
+
+        def add_bias(b, h, a):
+            result = rows_pool.tile([P, 2, UNITS], F32)
+            nc.vector.tensor_add(out=result[:], in0=acc[b, h, a][:], in1=bias[:])
+            nc.sync.dma_start(out=out_pairs[(b * BANKS + h) * 2 + a], in_=result[:])
+
+        chunks = [(b, c) for b in range(BLOCKS) for c in range(CHUNKS)]
+        steps = [chunk + (i,) for chunk in chunks for i in range(1, KNOTS - 1)]
+        TERMS = {
+            1: (0,), 2: (0, 1), 3: (0, 1), 4: (1, 4), 5: (4, 5), 6: (4, 5), 7: (4, 5), 8: (5,),
+        }
+        DONE = {5: (0, 1), 8: (4, 5)}
+
+        ALL_TILES = slice(0, TILES)
+
+        def at(r, rank, job, args):
+            jobs.setdefault((r, rank), []).append((job, args))
+
+        for k in range(PASSES):
+            at(6 + 2 * k, 8, group_weights, (k,))
+            at(6 + 2 * k + 1, 8, quantise_weights, (k,))
+        for r, s in enumerate(steps):
+            b, c, i = s
+            at(r, 2, square_of, s)
+            at(r + 2, 2, cube_of, s)
+            for j in TERMS[i]:
+                at(r + 3, 3, term_of, s + (j,))
+            if i == 4 or i == 5:
+                at(r + 3, 3, inner_term_of, s)
+            if i in (3, 4, 6, 7):
+                at(r + 4, 1, form_of, s)
+            if i in (6, 7):
+                at(r + 5, 1, inner_basis, (b, c, 2 if i == 6 else 3))
+            if i in DONE:
+                pair = DONE[i]
+                for h in range(BANKS):
+                    n = r + 5 + h
+                    at(n, 5, add_up, (b, c, pair, h))
+                    at(n + 2, 3, read_sum, (b, c, pair[0], h))
+                    n += 0
+                    at(n + 2, 3, read_sum, (b, c, pair[1], h))
+                    j = pair[1]
+                    if j == OUTER[-1]:
+                        for a in range(2):
+                            at(n + 2 + 1 + a, 6, transpose_back, (b, c, h, a))
+                            at(n + 2 + 2 + a, 3, regroup, (b, c, h, a))
+                        at(n + 7, 3, quantise, (b, h, 1 + c))
+                        if c == CHUNKS - 1:
+                            for a in range(2):
+                                at(n + 8 + 2 * a, 7, products, (b, h, a))
+                                at(n + 11 + 2 * a, 6, add_bias, (b, h, a))
+            if c == CHUNKS - 1 and i in (6, 7):
+                j = 2 if i == 6 else 3
+                for h in range(BANKS):
+                    at(r + 5 + 1 + h, 3, regroup_inner, (b, j, h))
+                    at(r + 10 + h, 3, quantise, (b, h, PASS_2 if j == 2 else PASS_3))
+            if c == 2 and i == 1:
+                for h in range(BANKS):
+                    at(r + 2 * h, 4, relu_branch, (b, h))
+                    at(r + 2 * h + 3, 3, quantise, (b, h, 0))
+            if i == 1 and c == 0 and b + 1 < BLOCKS:
+                bank = b + 1
+                at(r, 0, load_rows, (bank, ALL_TILES))
+                at(r + 6, 3, row_statistics, (bank, ALL_TILES))
+                for t in range(TILES):
+                    at(r + 10 + t, 4, normalise, (bank, t))
+                    at(r + 15 + 2 * t, 7, transpose_rows, (bank, t))
+                    at(r + 15 + 2 * t + 1, 4, gamma_beta, (bank, t))
+
+        one_tile = [slice(t, t + 1) for t in range(TILES)]
+        for tiles in one_tile:
+            load_rows(0, tiles)
+        for tiles in one_tile:
+            row_statistics(0, tiles)
 
         span = {}
         for s in (1, 2, 3, 4):
@@ -112,310 +421,17 @@ def tile_kanlinear_pa_t_kernel(
         nc.vector.tensor_copy(out=beta[:], in_=beta_bf[:])
         nc.vector.tensor_copy(out=bias[:, 0, :], in_=bias_bf[:])
         nc.vector.tensor_copy(out=bias[:, 1, :], in_=bias_bf[:])
-
-        w_codes = const.tile([P, PASSES, UNITS], U32, align_bytes=64)
-        w_scales = const.tile([P, PASSES, UNITS], U8, align_bytes=64)
-
-        def load_weights(pool):
-            w_raw = pool.tile([P, PASSES * PACK, UNITS], BF16, bufs=1)
-            nc.scalar.dma_start(out=w_raw[:, 0:PACK, :], in_=base_weight.rearrange("(t p) u -> p t u", p=P))
-            by_pair = spline_weight.rearrange("(c m e k) u -> c e m k u", c=CHUNKS, e=2, k=BASES)
-            for c in range(CHUNKS):
-                for o in range(2):
-                    for e in range(2):
-                        first = PACK * (1 + c) + e
-                        nc.scalar.dma_start(
-                            out=w_raw[o * P // 2 : (o + 1) * P // 2, first : first + 3 : 2, :],
-                            in_=by_pair[c, e, :, o : o + 5 : 4, :],
-                        )
-            by_basis = spline_weight.rearrange("(c p k) u -> k p c u", p=P, k=BASES)
-            for k, j in ((PASS_2, 2), (PASS_3, 3)):
-                nc.scalar.dma_start(out=w_raw[:, PACK * k : PACK * (k + 1), :], in_=by_basis[j])
-            return w_raw
-
-        def quantise_weights(pool, w_raw):
-            for k in range(PASSES):
-                w_grouped = pool.tile([P, UNITS, PACK], BF16, align_bytes=64)
-                nc.vector.tensor_copy(
-                    out=w_grouped[:], in_=w_raw[:, k * PACK : (k + 1) * PACK, :].rearrange("p t u -> p u t")
-                )
-                nc.vector.quantize_mx(
-                    out=w_codes[:, k, :].bitcast(FP8X4),
-                    scales=w_scales[:, k, :],
-                    in_=w_grouped[:].rearrange("p u t -> p (u t)"),
-                )
-
-        x_banks = x.rearrange("(b t p) f -> b p t f", t=TILES, p=P)
-        out_pairs = out.rearrange("(b t p) u -> b p t u", t=2, p=P)
-
-        x_sb, row_scale, row_shift, z, z_t, xn = {}, {}, {}, {}, {}, {}
-        square, cube, term, inner_term, form = {}, {}, {}, {}, {}
-        bank_sum, basis, inner, back, grouped = {}, {}, {}, {}, {}
-        codes, scales, acc = {}, {}, {}
-        pools, jobs = {}, {}
-
-        def roots_of(c):
-            nc.gpsimd.tensor_tensor(out=root[:, c, :], in0=factor[:, c, :], in1=half[:, c, :], op=ALU.pow)
-
-        def load_rows(bank):
-            x_sb[bank] = rows_pool.tile([P, TILES, FEATURES], BF16, name="x_sb")
-            nc.sync.dma_start(out=x_sb[bank][:], in_=x_banks[bank])
-
-        def row_statistics(bank):
-            stats = small.tile([P, TILES, 6], F32)
-            mean_var = small.tile([P, TILES, 2], F32)
-            for t in range(TILES):
-                nc.vector.bn_stats(out=stats[:, t, :], in_=x_sb[bank][:, t, :])
-            for t in range(TILES):
-                nc.vector.bn_aggr(out=mean_var[:, t, :], in_=stats[:, t, :])
-            var_eps = small.tile([P, TILES], F32)
-            nc.vector.tensor_scalar_add(out=var_eps[:], in0=mean_var[:, :, 1], scalar1=LN_EPS)
-            neg_mean = small.tile([P, TILES], F32)
-            nc.vector.tensor_scalar_mul(out=neg_mean[:], in0=mean_var[:, :, 0], scalar1=-1.0)
-            row_scale[bank] = small.tile([P, TILES], F32, name="row_scale")
-            nc.gpsimd.tensor_tensor(out=row_scale[bank][:], in0=var_eps[:], in1=neg_half[:], op=ALU.pow)
-            row_shift[bank] = small.tile([P, TILES], F32, name="row_shift")
-            nc.gpsimd.tensor_tensor(out=row_shift[bank][:], in0=neg_mean[:], in1=row_scale[bank][:], op=ALU.mult)
-
-        def normalise(bank, t):
-            if t == 0:
-                z[bank] = rows_pool.tile([P, TILES, FEATURES], F32, name="z", bufs=1)
-            nc.scalar.activation(
-                out=z[bank][:, t, :], in_=x_sb[bank][:, t, :], func=ACT.Identity,
-                scale=row_scale[bank][:, t : t + 1], bias=row_shift[bank][:, t : t + 1],
-            )
-
-        def transpose_rows(bank, c):
-            z_t[bank, c] = psum.tile([P, BANK], F32, name="z_t", tag="misc")
-            for t in range(TILES):
-                nc.tensor.transpose(
-                    z_t[bank, c][:, t * P : (t + 1) * P], z[bank][:, t, c * P : (c + 1) * P], ident[:]
-                )
-
-        def gamma_beta(bank, c):
-            b, h = divmod(bank, BANKS)
-            if h == 0 and c == 0:
-                xn[b] = xn_pool.tile([P, CHUNKS, BLOCK], F32, name="xn")
-            nc.scalar.activation(
-                out=xn[b][:, c, h * BANK : (h + 1) * BANK], in_=z_t[bank, c][:], func=ACT.Identity,
-                scale=gamma[:, c : c + 1], bias=beta[:, c : c + 1],
-            )
-
-        def new_group(b, h, k):
-            grouped[b, h, k] = planes.tile([P, BANK, PACK], BF16, align_bytes=64, name="grouped", bufs=6)
-            return grouped[b, h, k]
-
-        def relu_branch(b, h):
-            nc.scalar.activation(
-                out=new_group(b, h, 0)[:],
-                in_=xn[b][:, :, h * BANK : (h + 1) * BANK].rearrange("p t n -> p n t"), func=ACT.Relu,
-            )
-
-        def quantise(b, h, k):
-            if (b, h) not in codes:
-                codes[b, h] = mx.tile([P, PASSES, BANK], U32, align_bytes=64, name="codes")
-                scales[b, h] = mx.tile([P, PASSES, BANK], U8, align_bytes=64, name="scales")
-            nc.vector.quantize_mx(
-                out=codes[b, h][:, k, :].bitcast(FP8X4), scales=scales[b, h][:, k, :],
-                in_=grouped[b, h, k][:].rearrange("p n t -> p (n t)"),
-            )
-
-        def square_of(b, c, i):
-            square[b, c, i] = pools["work"].tile([P, BLOCK], F32, name="square", bufs=4)
-            nc.scalar.activation(
-                out=square[b, c, i][:], in_=xn[b][:, c, :], func=ACT.Square,
-                scale=root[:, c, i : i + 1], bias=root_shift[:, c, i : i + 1],
-            )
-
-        def cube_of(b, c, i):
-            cube[b, c, i] = pools["work"].tile([P, BLOCK], F32, name="cube", bufs=10)
-            nc.vector.scalar_tensor_tensor(
-                out=cube[b, c, i][:], in0=xn[b][:, c, :], scalar=knots[:, c, i : i + 1], in1=square[b, c, i][:],
-                op0=ALU.subtract, op1=ALU.mult,
-            )
-
-        def term_of(b, c, i, j):
-            k = i - j
-            term[b, c, j, k] = pools["work"].tile([P, BLOCK], F32, name="term", bufs=20)
-            dst, src, scale = term[b, c, j, k][:], cube[b, c, i][:], coef[k][:, c, j : j + 1]
-            if k == 0:
-                nc.vector.tensor_scalar_mul(out=dst, in0=src, scalar1=scale)
-            elif (j, k) in SCALAR_TERMS:
-                nc.scalar.activation(out=dst, in_=src, func=ACT.Relu, scale=scale)
-            else:
-                nc.vector.tensor_scalar(
-                    out=dst, in0=src, scalar1=0.0, scalar2=scale, op0=ALU.min if j < 2 else ALU.max, op1=ALU.mult
-                )
-
-        def add_up(b, c, j, h):
-            bank_sum[b, c, j, h] = psum.tile([P, BANK], F32, name="bank_sum", tag="sum", bufs=4)
-            if j < 2:
-                parts = [cube[b, c, j + 4]] + [term[b, c, j, k] for k in (3, 2, 1)]
-            else:
-                parts = [term[b, c, j, k] for k in (0, 1, 2, 3)]
-            for t in range(TILES):
-                rows = slice(h * BANK + t * P, h * BANK + (t + 1) * P)
-                for n, part in enumerate(parts):
-                    nc.tensor.matmul(
-                        bank_sum[b, c, j, h][:, t * P : (t + 1) * P], lhsT=part[:, rows], rhs=ident[:],
-                        is_transpose=True, start=(n == 0), stop=(n == 3),
-                    )
-
-        def read_sum(b, c, j, h):
-            if j == OUTER[0] and h == 0:
-                basis[b, c] = planes.tile([P, BANKS, TILES, len(OUTER), P], BF16, name="basis")
-            nc.scalar.activation(
-                out=basis[b, c][:, h, :, OUTER.index(j), :],
-                in_=bank_sum[b, c, j, h][:].rearrange("p (t f) -> p t f", f=P),
-                func=ACT.Relu, scale=-1.0 if j < 2 else 1.0,
-            )
-
-        def transpose_back(b, c, h, a):
-            back[b, c, h, a] = psum.tile([P, 2, 2, P], F32, name="back", tag="back")
-            for u in range(2):
-                for t in range(2):
-                    words = basis[b, c][:, h, 2 * a + t, 2 * u : 2 * u + 2, :]
-                    nc.tensor.transpose(
-                        back[b, c, h, a][:, u, t, :], words.rearrange("p j f -> p (j f)").bitcast(F32), ident[:]
-                    )
-
-        def regroup(b, c, h, a):
-            if a == 0:
-                new_group(b, h, 1 + c)
-            dst = grouped[b, h, 1 + c][:].rearrange("p n t -> p (n t)").bitcast(F32)
-            dst = dst[:, a * BANK : (a + 1) * BANK].rearrange("p (n u) -> p n u", u=2)
-            nc.scalar.copy(out=dst, in_=back[b, c, h, a][:].rearrange("p u t n -> p (t n) u"))
-
-        def inner_term_of(b, c, i):
-            inner_term[b, c, i] = pools["work"].tile([P, BLOCK], F32, name="inner_term", bufs=2)
-            j, k = (3, 1) if i == 4 else (2, 3)
-            nc.vector.tensor_scalar(
-                out=inner_term[b, c, i][:], in0=cube[b, c, i][:], scalar1=0.0, scalar2=coef[k][:, c, j : j + 1],
-                op0=ALU.max if i == 4 else ALU.min, op1=ALU.mult,
-            )
-
-        def form_of(b, c, i):
-            form[b, c, i] = planes.tile([P, BLOCK], BF16, name="form", bufs=6)
-            dst = form[b, c, i][:]
-            if i == 3:
-                nc.vector.scalar_tensor_tensor(
-                    out=dst, in0=cube[b, c, 3][:], scalar=0.0, in1=cube[b, c, 2][:], op0=ALU.max, op1=ALU.subtract
-                )
-            elif i == 7:
-                nc.vector.scalar_tensor_tensor(
-                    out=dst, in0=cube[b, c, 6][:], scalar=0.0, in1=cube[b, c, 7][:], op0=ALU.min, op1=ALU.subtract
-                )
-            else:
-                source, j, k = (3, 3, 0) if i == 4 else (6, 2, 4)
-                nc.vector.scalar_tensor_tensor(
-                    out=dst, in0=cube[b, c, source][:], scalar=coef[k][:, c, j : j + 1],
-                    in1=inner_term[b, c, i if i == 4 else 5][:], op0=ALU.mult, op1=ALU.add,
-                )
-
-        def inner_basis(b, c, j):
-            if c == 0:
-                inner[b, j] = planes.tile([P, CHUNKS, BLOCK], BF16, name="inner%d" % j, bufs=1)
-            nc.vector.tensor_tensor(
-                out=inner[b, j][:, c, :], in0=form[b, c, 3 if j == 2 else 4][:], in1=form[b, c, 6 if j == 2 else 7][:],
-                op=ALU.min if j == 2 else ALU.max,
-            )
-
-        def regroup_inner(b, j, h):
-            dst = new_group(b, h, PASS_2 if j == 2 else PASS_3)[:].rearrange("p (a i) t -> p a t i", i=4)
-            src = inner[b, j][:, :, h * BANK : (h + 1) * BANK].rearrange("p t (a i) -> p a t i", i=4)
-            nc.scalar.activation(out=dst, in_=src, func=ACT.Relu, scale=-1.0 if j == 2 else 1.0)
-
-        def products(b, h, a):
-            acc[b, h, a] = psum.tile([P, 2, UNITS], F32, name="acc", tag="misc")
-            for t in range(2):
-                cols = slice((2 * a + t) * P, (2 * a + t + 1) * P)
-                for k in range(PASSES):
-                    nc.tensor.matmul_mx(
-                        out=acc[b, h, a][:, t, :],
-                        lhsT=codes[b, h][:, k, cols].bitcast(FP8X4), lhsT_scale=scales[b, h][:, k, cols],
-                        rhs=w_codes[:, k, :].bitcast(FP8X4), rhs_scale=w_scales[:, k, :],
-                        start=(k == 0), stop=(k == PASSES - 1),
-                    )
-
-        def add_bias(b, h, a):
-            result = rows_pool.tile([P, 2, UNITS], F32)
-            nc.vector.tensor_add(out=result[:], in0=acc[b, h, a][:], in1=bias[:])
-            nc.sync.dma_start(out=out_pairs[(b * BANKS + h) * 2 + a], in_=result[:])
-
-        chunks = [(b, c) for b in range(BLOCKS) for c in range(CHUNKS)]
-        steps = [chunk + (i,) for chunk in chunks for i in range(1, KNOTS - 1)]
-        TERMS = {
-            1: (0,), 2: (0, 1), 3: (0, 1), 4: (1, 4), 5: (4, 5), 6: (4, 5), 7: (4, 5), 8: (5,),
-        }
-        DONE = {4: 0, 5: 1, 7: 4, 8: 5}
-
-        def at(r, rank, job, args):
-            jobs.setdefault((r, rank), []).append((job, args))
-
-        for r, s in enumerate(steps):
-            b, c, i = s
-            at(r, 2, square_of, s)
-            at(r + 2, 2, cube_of, s)
-            for j in TERMS[i]:
-                at(r + 3, 3, term_of, s + (j,))
-            if i == 4 or i == 5:
-                at(r + 3, 3, inner_term_of, s)
-            if i in (3, 4, 6, 7):
-                at(r + 4, 1, form_of, s)
-            if i in (6, 7):
-                at(r + 5, 1, inner_basis, (b, c, 2 if i == 6 else 3))
-            if i in DONE:
-                j = DONE[i]
-                for h in range(BANKS):
-                    n = r + (5, 6, 6, 7)[OUTER.index(j)] + h
-                    at(n, 5, add_up, (b, c, j, h))
-                    at(n + 2, 1, read_sum, (b, c, j, h))
-                    if j == OUTER[-1]:
-                        for a in range(2):
-                            at(n + 2 + 1 + a, 6, transpose_back, (b, c, h, a))
-                            at(n + 2 + 2 + a, 3, regroup, (b, c, h, a))
-                        at(n + 2 + 4, 3, quantise, (b, h, 1 + c))
-                        if c == CHUNKS - 1:
-                            for a in range(2):
-                                at(n + 2 + 5 + a, 7, products, (b, h, a))
-                                at(n + 2 + 6 + a, 6, add_bias, (b, h, a))
-            if c == CHUNKS - 1 and i in (6, 7):
-                j = 2 if i == 6 else 3
-                for h in range(BANKS):
-                    at(r + 5 + 1 + h, 3, regroup_inner, (b, j, h))
-                    at(r + 10 + h, 3, quantise, (b, h, PASS_2 if j == 2 else PASS_3))
-            if c == 2 and i == 1:
-                for h in range(BANKS):
-                    at(r + 2 * h, 4, relu_branch, (b, h))
-                    at(r + 2 * h + 3, 3, quantise, (b, h, 0))
-            if i == 1 and c == 0 and b + 1 < BLOCKS:
-                bank = b + 1
-                at(r, 0, load_rows, (bank,))
-                at(r + 6, 3, row_statistics, (bank,))
-                for t in range(TILES):
-                    at(r + 10 + t, 4, normalise, (bank, t))
-                    at(r + 15 + 2 * t, 7, transpose_rows, (bank, t))
-                    at(r + 15 + 2 * t + 1, 4, gamma_beta, (bank, t))
-
-        for bank in range(BANKS):
-            load_rows(bank)
         roots_of(0)
-        with tc.tile_pool(name="wprep", bufs=2) as wprep:
-            w_raw = load_weights(wprep)
-            for bank in range(BANKS):
-                row_statistics(bank)
-            for c in range(1, CHUNKS):
-                roots_of(c)
-            nc.vector.tensor_mul(out=root_shift[:, 0, :], in0=root[:, 0, :], in1=neg_knots[:, 0, :])
-            quantise_weights(wprep, w_raw)
-            nc.vector.tensor_mul(out=root_shift[:, 1:, :], in0=root[:, 1:, :], in1=neg_knots[:, 1:, :])
-        pools["work"] = ctx.enter_context(tc.tile_pool(name="work", bufs=2, reuse_waits="tile"))
-        for bank in range(BANKS):
-            for t in range(TILES):
-                normalise(bank, t)
-            for c in range(CHUNKS):
-                transpose_rows(bank, c)
-                gamma_beta(bank, c)
+        nc.vector.tensor_mul(out=root_shift[:, 0, :], in0=root[:, 0, :], in1=neg_knots[:, 0, :])
+        w_raw = load_weights()
+        for c in range(1, CHUNKS):
+            roots_of(c)
+        nc.vector.tensor_mul(out=root_shift[:, 1:, :], in0=root[:, 1:, :], in1=neg_knots[:, 1:, :])
+        for t in range(TILES):
+            normalise(0, t)
+        for c in range(CHUNKS):
+            transpose_rows(0, c)
+            gamma_beta(0, c)
         ctx.enter_context(tc.manual_schedule())
         for key in sorted(jobs):
             for job, args in jobs[key]:

@@ -114,6 +114,9 @@ def tile_kanlinear_pa_t_kernel(
         def roots_of(c):
             nc.gpsimd.tensor_tensor(out=root[:, c, :], in0=factor[:, c, :], in1=half[:, c, :], op=ALU.pow)
 
+        def shifts_of(c):
+            nc.vector.tensor_mul(out=root_shift[:, c, :], in0=root[:, c, :], in1=neg_knots[:, c, :])
+
         def load_rows(bank, tiles):
             if bank not in x_sb:
                 x_sb[bank] = rows_pool.tile([P, TILES, FEATURES], BF16, name="x_sb")
@@ -210,22 +213,19 @@ def tile_kanlinear_pa_t_kernel(
                     out=dst, in0=src, scalar1=0.0, scalar2=scale, op0=ALU.min if j < 2 else ALU.max, op1=ALU.mult
                 )
 
-        def add_up(b, c, pair, h):
-            parts = {}
-            for j in pair:
-                bank_sum[b, c, j, h] = psum.tile([P, BANK], F32, name="bank_sum", tag="sum", bufs=4)
-                if j < 2:
-                    parts[j] = [cube[b, c, j + 4]] + [term[b, c, j, k] for k in (3, 2, 1)]
-                else:
-                    parts[j] = [term[b, c, j, k] for k in (0, 1, 2, 3)]
+        def add_up(b, c, j, h):
+            bank_sum[b, c, j, h] = psum.tile([P, BANK], F32, name="bank_sum", tag="sum", bufs=4)
+            if j < 2:
+                parts = [cube[b, c, j + 4]] + [term[b, c, j, k] for k in (3, 2, 1)]
+            else:
+                parts = [term[b, c, j, k] for k in (0, 1, 2, 3)]
             for t in range(TILES):
                 rows = slice(h * BANK + t * P, h * BANK + (t + 1) * P)
-                for n in range(4):
-                    for j in pair:
-                        nc.tensor.matmul(
-                            bank_sum[b, c, j, h][:, t * P : (t + 1) * P], lhsT=parts[j][n][:, rows], rhs=ident[:],
-                            is_transpose=True, start=(n == 0), stop=(n == 3),
-                        )
+                for n, part in enumerate(parts):
+                    nc.tensor.matmul(
+                        bank_sum[b, c, j, h][:, t * P : (t + 1) * P], lhsT=part[:, rows], rhs=ident[:],
+                        is_transpose=True, start=(n == 0), stop=(n == 3),
+                    )
 
         def read_sum(b, c, j, h):
             if j == OUTER[0] and h == 0:
@@ -313,13 +313,15 @@ def tile_kanlinear_pa_t_kernel(
         TERMS = {
             1: (0,), 2: (0, 1), 3: (0, 1), 4: (1, 4), 5: (4, 5), 6: (4, 5), 7: (4, 5), 8: (5,),
         }
-        DONE = {5: (0, 1), 8: (4, 5)}
+        DONE = {4: 0, 5: 1, 7: 4, 8: 5}
 
         ALL_TILES = slice(0, TILES)
 
         def at(r, rank, job, args):
             jobs.setdefault((r, rank), []).append((job, args))
 
+        for c in range(1, CHUNKS):
+            at(3, 8, shifts_of, (c,))
         for k in range(PASSES):
             at(6 + 2 * k, 8, group_weights, (k,))
             at(6 + 2 * k + 1, 8, quantise_weights, (k,))
@@ -336,14 +338,11 @@ def tile_kanlinear_pa_t_kernel(
             if i in (6, 7):
                 at(r + 5, 1, inner_basis, (b, c, 2 if i == 6 else 3))
             if i in DONE:
-                pair = DONE[i]
+                j = DONE[i]
                 for h in range(BANKS):
-                    n = r + 5 + h
-                    at(n, 5, add_up, (b, c, pair, h))
-                    at(n + 2, 3, read_sum, (b, c, pair[0], h))
-                    n += 0
-                    at(n + 2, 3, read_sum, (b, c, pair[1], h))
-                    j = pair[1]
+                    n = r + (5, 6, 6, 7)[OUTER.index(j)] + h
+                    at(n, 5, add_up, (b, c, j, h))
+                    at(n + 2, 1, read_sum, (b, c, j, h))
                     if j == OUTER[-1]:
                         for a in range(2):
                             at(n + 2 + 1 + a, 6, transpose_back, (b, c, h, a))
@@ -422,11 +421,10 @@ def tile_kanlinear_pa_t_kernel(
         nc.vector.tensor_copy(out=bias[:, 0, :], in_=bias_bf[:])
         nc.vector.tensor_copy(out=bias[:, 1, :], in_=bias_bf[:])
         roots_of(0)
-        nc.vector.tensor_mul(out=root_shift[:, 0, :], in0=root[:, 0, :], in1=neg_knots[:, 0, :])
+        shifts_of(0)
         w_raw = load_weights()
         for c in range(1, CHUNKS):
             roots_of(c)
-        nc.vector.tensor_mul(out=root_shift[:, 1:, :], in0=root[:, 1:, :], in1=neg_knots[:, 1:, :])
         for t in range(TILES):
             normalise(0, t)
         for c in range(CHUNKS):

@@ -376,6 +376,14 @@ def tile_kanlinear_pa_t_kernel(
         for tiles in one_tile:
             row_statistics(0, tiles)
 
+        gamma = const.tile([P, CHUNKS], F32)
+        beta = const.tile([P, CHUNKS], F32)
+        bias = const.tile([P, 2, UNITS], F32)
+        nc.vector.tensor_copy(out=gamma[:], in_=gamma_bf[:])
+        nc.vector.tensor_copy(out=beta[:], in_=beta_bf[:])
+        nc.vector.tensor_copy(out=bias[:, 0, :], in_=bias_bf[:])
+        nc.vector.tensor_copy(out=bias[:, 1, :], in_=bias_bf[:])
+
         span = {}
         for s in (1, 2, 3, 4):
             span[s] = const.tile([P, CHUNKS, KNOTS - s], F32, name="span%d" % s)
@@ -413,13 +421,6 @@ def tile_kanlinear_pa_t_kernel(
             coef[k] = const.tile([P, CHUNKS, BASES], F32, name="coef%d" % k)
             nc.vector.tensor_mul(out=coef[k][:], in0=weight[k][:], in1=inv_factor[:, :, k : k + BASES])
 
-        gamma = const.tile([P, CHUNKS], F32)
-        beta = const.tile([P, CHUNKS], F32)
-        bias = const.tile([P, 2, UNITS], F32)
-        nc.vector.tensor_copy(out=gamma[:], in_=gamma_bf[:])
-        nc.vector.tensor_copy(out=beta[:], in_=beta_bf[:])
-        nc.vector.tensor_copy(out=bias[:, 0, :], in_=bias_bf[:])
-        nc.vector.tensor_copy(out=bias[:, 1, :], in_=bias_bf[:])
         roots_of(0)
         shifts_of(0)
         w_raw = load_weights()
@@ -430,7 +431,6 @@ def tile_kanlinear_pa_t_kernel(
         for c in range(CHUNKS):
             transpose_rows(0, c)
             gamma_beta(0, c)
-        ctx.enter_context(tc.manual_schedule())
         for key in sorted(jobs):
             for job, args in jobs[key]:
                 job(*args)

@@ -28,7 +28,7 @@ BANK = 512
 TILES = BANK // P
 BANKS = BLOCK // BANK
 LN_EPS = 0.001
-SCALAR_TERMS = ((0, 3), (1, 3), (4, 2), (5, 2))
+SCALAR_TERMS = ((0, 3), (1, 3), (4, 2), (5, 2), (1, 1))
 
 FLOPS = 2 * ROWS * (FEATURES + FEATURES * BASES) * UNITS
 
@@ -203,7 +203,8 @@ def tile_kanlinear_pa_t_kernel(
         def term_of(b, c, i, j):
             k = i - j
             term[b, c, j, k] = work.tile([P, BLOCK], F32, name="term", bufs=22)
-            dst, src, scale = term[b, c, j, k][:], cube[b, c, i][:], coef[k][:, c, j : j + 1]
+            dst, src = term[b, c, j, k][:], cube[b, c, i][:]
+            scale = -1.0 if i in (1, 8) else coef[k][:, c, j : j + 1]
             if k == 0:
                 nc.vector.tensor_scalar_mul(out=dst, in0=src, scalar1=scale)
             elif (j, k) in SCALAR_TERMS:
@@ -404,7 +405,9 @@ def tile_kanlinear_pa_t_kernel(
             if k % 2 == 1:
                 nc.vector.tensor_scalar_mul(out=weight[k][:], in0=weight[k][:], scalar1=-1.0)
 
-        FACTORS = {2: (0, 2, 1), 3: (1, 2, -1), 4: (4, 0, 1), 5: (4, 1, 1), 6: (3, 3, -1), 7: (4, 3, 1)}
+        FACTORS = {
+            1: (1, 0, -1), 2: (0, 2, 1), 3: (1, 2, -1), 4: (4, 0, 1), 5: (4, 1, 1), 6: (3, 3, -1), 7: (4, 3, 1), 8: (3, 5, -1),
+        }
         factor = const.tile([P, CHUNKS, KNOTS], F32)
         nc.vector.memset(factor[:], 1.0)
         for i in FACTORS:

from contextlib import ExitStack

import concourse.mybir as mybir
from concourse.masks import make_identity

F32 = mybir.dt.float32
BF16 = mybir.dt.bfloat16
U32 = mybir.dt.uint32
U8 = mybir.dt.uint8
FP8X4 = mybir.dt.float8_e4m3fn_x4
ALU = mybir.AluOpType
ACT = mybir.ActivationFunctionType

P = 128
PACK = 4
ROWS = 4096
FEATURES = 512
UNITS = 256
KNOTS = 10
BASES = 6
CHUNKS = FEATURES // P
OUTER = (0, 1, 4, 5)
PASSES = 1 + CHUNKS + 2
PASS_2, PASS_3 = 1 + CHUNKS, 2 + CHUNKS
BLOCK = 512
BLOCKS = ROWS // BLOCK
BANK = 512
TILES = BANK // P
BANKS = BLOCK // BANK
LN_EPS = 0.001
SCALAR_TERMS = ((0, 3), (1, 3), (4, 2), (5, 2), (1, 1))

FLOPS = 2 * ROWS * (FEATURES + FEATURES * BASES) * UNITS


def tile_kanlinear_pa_t_kernel(
    tc, x, ln_gamma, ln_beta, base_weight, base_bias, spline_weight, grid, out
):
    nc = tc.nc
    with ExitStack() as ctx:
        const = ctx.enter_context(tc.tile_pool(name="const", bufs=1))
        rows_pool = ctx.enter_context(tc.tile_pool(name="rows", bufs=2))
        small = ctx.enter_context(tc.tile_pool(name="small", bufs=2))
        xn_pool = ctx.enter_context(tc.tile_pool(name="xn", bufs=2))
        planes = ctx.enter_context(tc.tile_pool(name="planes", bufs=2))
        mx = ctx.enter_context(tc.tile_pool(name="mx", bufs=2))
        work = ctx.enter_context(tc.tile_pool(name="work", bufs=2))
        psum = ctx.enter_context(tc.psum_pool(name="psum", bufs=2))

        ident = const.tile([P, P], F32)
        make_identity(nc, ident[:])

        knots_bf = const.tile([P, CHUNKS, KNOTS], BF16)
        nc.scalar.dma_start(out=knots_bf[:], in_=grid.rearrange("o (c p) t -> p (o c) t", p=P))
        gamma_bf = const.tile([P, CHUNKS], BF16)
        beta_bf = const.tile([P, CHUNKS], BF16)
        with nc.allow_non_contiguous_dma(reason="512 elements, one per partition and chunk"):
            nc.scalar.dma_start(out=gamma_bf[:], in_=ln_gamma.rearrange("(c p) -> p c", p=P))
            nc.scalar.dma_start(out=beta_bf[:], in_=ln_beta.rearrange("(c p) -> p c", p=P))
        bias_bf = const.tile([P, UNITS], BF16)
        nc.scalar.dma_start(out=bias_bf[:], in_=base_bias.partition_broadcast(P))

        knots = const.tile([P, CHUNKS, KNOTS], F32)
        nc.vector.tensor_copy(out=knots[:], in_=knots_bf[:])
        half = const.tile([P, CHUNKS, KNOTS], F32)
        nc.vector.memset(half[:], 0.5)
        neg_half = const.tile([P, TILES], F32)
        nc.vector.memset(neg_half[:], -0.5)
        neg_knots = const.tile([P, CHUNKS, KNOTS], F32)
        nc.vector.tensor_scalar_mul(out=neg_knots[:], in0=knots[:], scalar1=-1.0)

        w_codes = const.tile([P, PASSES, UNITS], U32, align_bytes=64)
        w_scales = const.tile([P, PASSES, UNITS], U8, align_bytes=64)

        def load_weights():
            w_raw = const.tile([P, PASSES * PACK, UNITS], BF16)
            nc.sync.dma_start(out=w_raw[:, 0:PACK, :], in_=base_weight.rearrange("(t p) u -> p t u", p=P))
            by_pair = spline_weight.rearrange("(c m e k) u -> c e m k u", c=CHUNKS, e=2, k=BASES)
            for c in range(CHUNKS):
                for o in range(2):
                    for e in range(2):
                        first = PACK * (1 + c) + e
                        nc.sync.dma_start(
                            out=w_raw[o * P // 2 : (o + 1) * P // 2, first : first + 3 : 2, :],
                            in_=by_pair[c, e, :, o : o + 5 : 4, :],
                        )
            by_basis = spline_weight.rearrange("(c p k) u -> k p c u", p=P, k=BASES)
            for k, j in ((PASS_2, 2), (PASS_3, 3)):
                nc.sync.dma_start(out=w_raw[:, PACK * k : PACK * (k + 1), :], in_=by_basis[j])
            return w_raw

        def group_weights(k):
            w_grouped[k] = small.tile([P, UNITS, PACK], BF16, name="w_grouped", align_bytes=64)
            nc.vector.tensor_copy(
                out=w_grouped[k][:], in_=w_raw[:, k * PACK : (k + 1) * PACK, :].rearrange("p t u -> p u t")
            )

        def quantise_weights(k):
            nc.vector.quantize_mx(
                out=w_codes[:, k, :].bitcast(FP8X4),
                scales=w_scales[:, k, :],
                in_=w_grouped[k][:].rearrange("p u t -> p (u t)"),
            )

        x_banks = x.rearrange("(b t p) f -> b p t f", t=TILES, p=P)
        out_pairs = out.rearrange("(b t p) u -> b p t u", t=2, p=P)

        x_sb, row_scale, row_shift, z, z_t, xn = {}, {}, {}, {}, {}, {}
        square, cube, term, inner_term, form = {}, {}, {}, {}, {}
        bank_sum, basis, inner, back, grouped = {}, {}, {}, {}, {}
        codes, scales, acc, w_grouped = {}, {}, {}, {}
        jobs = {}

        def roots_of(c):
            nc.gpsimd.tensor_tensor(out=root[:, c, :], in0=factor[:, c, :], in1=half[:, c, :], op=ALU.pow)

        def shifts_of(c):
            nc.vector.tensor_mul(out=root_shift[:, c, :], in0=root[:, c, :], in1=neg_knots[:, c, :])

        def load_rows(bank, tiles):
            if bank not in x_sb:
                x_sb[bank] = rows_pool.tile([P, TILES, FEATURES], BF16, name="x_sb")
            nc.sync.dma_start(out=x_sb[bank][:, tiles, :], in_=x_banks[bank][:, tiles, :])

        def row_statistics(bank, tiles):
            if bank not in row_scale:
                row_scale[bank] = small.tile([P, TILES], F32, name="row_scale")
                row_shift[bank] = small.tile([P, TILES], F32, name="row_shift")
            stats = small.tile([P, TILES, 6], F32)
            mean_var = small.tile([P, TILES, 2], F32)
            for t in range(tiles.start, tiles.stop):
                nc.vector.bn_stats(out=stats[:, t, :], in_=x_sb[bank][:, t, :])
            for t in range(tiles.start, tiles.stop):
                nc.vector.bn_aggr(out=mean_var[:, t, :], in_=stats[:, t, :])
            var_eps = small.tile([P, TILES], F32)
            nc.vector.tensor_scalar_add(out=var_eps[:, tiles], in0=mean_var[:, tiles, 1], scalar1=LN_EPS)
            neg_mean = small.tile([P, TILES], F32)
            nc.vector.tensor_scalar_mul(out=neg_mean[:, tiles], in0=mean_var[:, tiles, 0], scalar1=-1.0)
            nc.gpsimd.tensor_tensor(
                out=row_scale[bank][:, tiles], in0=var_eps[:, tiles], in1=neg_half[:, tiles], op=ALU.pow
            )
            nc.gpsimd.tensor_tensor(
                out=row_shift[bank][:, tiles], in0=neg_mean[:, tiles], in1=row_scale[bank][:, tiles], op=ALU.mult
            )

        def normalise(bank, t):
            if t == 0:
                z[bank] = rows_pool.tile([P, TILES, FEATURES], F32, name="z", bufs=1)
            nc.scalar.activation(
                out=z[bank][:, t, :], in_=x_sb[bank][:, t, :], func=ACT.Identity,
                scale=row_scale[bank][:, t : t + 1], bias=row_shift[bank][:, t : t + 1],
            )

        def transpose_rows(bank, c):
            z_t[bank, c] = psum.tile([P, BANK], F32, name="z_t", tag="back")
            for t in range(TILES):
                nc.tensor.transpose(
                    z_t[bank, c][:, t * P : (t + 1) * P], z[bank][:, t, c * P : (c + 1) * P], ident[:]
                )

        def gamma_beta(bank, c):
            b, h = divmod(bank, BANKS)
            if h == 0 and c == 0:
                xn[b] = xn_pool.tile([P, CHUNKS, BLOCK], F32, name="xn")
            nc.scalar.activation(
                out=xn[b][:, c, h * BANK : (h + 1) * BANK], in_=z_t[bank, c][:], func=ACT.Identity,
                scale=gamma[:, c : c + 1], bias=beta[:, c : c + 1],
            )

        def new_group(b, h, k):
            grouped[b, h, k] = planes.tile([P, BANK, PACK], BF16, align_bytes=64, name="grouped", bufs=7)
            return grouped[b, h, k]

        def relu_branch(b, h):
            nc.scalar.activation(
                out=new_group(b, h, 0)[:],
                in_=xn[b][:, :, h * BANK : (h + 1) * BANK].rearrange("p t n -> p n t"), func=ACT.Relu,
            )

        def quantise(b, h, k):
            if (b, h) not in codes:
                codes[b, h] = mx.tile([P, PASSES, BANK], U32, align_bytes=64, name="codes")
                scales[b, h] = mx.tile([P, PASSES, BANK], U8, align_bytes=64, name="scales")
            nc.vector.quantize_mx(
                out=codes[b, h][:, k, :].bitcast(FP8X4), scales=scales[b, h][:, k, :],
                in_=grouped[b, h, k][:].rearrange("p n t -> p (n t)"),
            )

        def square_of(b, c, i):
            square[b, c, i] = work.tile([P, BLOCK], F32, name="square", bufs=4)
            nc.scalar.activation(
                out=square[b, c, i][:], in_=xn[b][:, c, :], func=ACT.Square,
                scale=root[:, c, i : i + 1], bias=root_shift[:, c, i : i + 1],
            )

        def cube_of(b, c, i):
            cube[b, c, i] = work.tile([P, BLOCK], F32, name="cube", bufs=10)
            nc.vector.scalar_tensor_tensor(
                out=cube[b, c, i][:], in0=xn[b][:, c, :], scalar=knots[:, c, i : i + 1], in1=square[b, c, i][:],
                op0=ALU.subtract, op1=ALU.mult,
            )

        def term_of(b, c, i, j):
            k = i - j
            term[b, c, j, k] = work.tile([P, BLOCK], F32, name="term", bufs=22)
            dst, src = term[b, c, j, k][:], cube[b, c, i][:]
            scale = -1.0 if i in (1, 8) else coef[k][:, c, j : j + 1]
            if k == 0:
                nc.vector.tensor_scalar_mul(out=dst, in0=src, scalar1=scale)
            elif (j, k) in SCALAR_TERMS:
                nc.scalar.activation(out=dst, in_=src, func=ACT.Relu, scale=scale)
            else:
                nc.vector.tensor_scalar(
                    out=dst, in0=src, scalar1=0.0, scalar2=scale, op0=ALU.min if j < 2 else ALU.max, op1=ALU.mult
                )

        def add_up(b, c, j, h):
            bank_sum[b, c, j, h] = psum.tile([P, BANK], F32, name="bank_sum", tag="sum", bufs=4)
            if j < 2:
                parts = [cube[b, c, j + 4]] + [term[b, c, j, k] for k in (3, 2, 1)]
            else:
                parts = [term[b, c, j, k] for k in (0, 1, 2, 3)]
            for t in range(TILES):
                rows = slice(h * BANK + t * P, h * BANK + (t + 1) * P)
                for n, part in enumerate(parts):
                    nc.tensor.matmul(
                        bank_sum[b, c, j, h][:, t * P : (t + 1) * P], lhsT=part[:, rows], rhs=ident[:],
                        is_transpose=True, start=(n == 0), stop=(n == 3),
                    )

        def read_sum(b, c, j, h):
            if j == OUTER[0] and h == 0:
                basis[b, c] = planes.tile([P, BANKS, TILES, len(OUTER), P], BF16, name="basis")
            nc.scalar.activation(
                out=basis[b, c][:, h, :, OUTER.index(j), :],
                in_=bank_sum[b, c, j, h][:].rearrange("p (t f) -> p t f", f=P),
                func=ACT.Relu, scale=-1.0 if j < 2 else 1.0,
            )

        def transpose_back(b, c, h, a):
            back[b, c, h, a] = psum.tile([P, 2, 2, P], F32, name="back", tag="back")
            for u in range(2):
                for t in range(2):
                    words = basis[b, c][:, h, 2 * a + t, 2 * u : 2 * u + 2, :]
                    nc.tensor.transpose(
                        back[b, c, h, a][:, u, t, :], words.rearrange("p j f -> p (j f)").bitcast(F32), ident[:]
                    )

        def regroup(b, c, h, a):
            if a == 0:
                new_group(b, h, 1 + c)
            dst = grouped[b, h, 1 + c][:].rearrange("p n t -> p (n t)").bitcast(F32)
            dst = dst[:, a * BANK : (a + 1) * BANK].rearrange("p (n u) -> p n u", u=2)
            nc.scalar.copy(out=dst, in_=back[b, c, h, a][:].rearrange("p u t n -> p (t n) u"))

        def inner_term_of(b, c, i):
            inner_term[b, c, i] = work.tile([P, BLOCK], F32, name="inner_term", bufs=2)
            j, k = (3, 1) if i == 4 else (2, 3)
            nc.vector.tensor_scalar(
                out=inner_term[b, c, i][:], in0=cube[b, c, i][:], scalar1=0.0, scalar2=coef[k][:, c, j : j + 1],
                op0=ALU.max if i == 4 else ALU.min, op1=ALU.mult,
            )

        def form_of(b, c, i):
            form[b, c, i] = planes.tile([P, BLOCK], BF16, name="form", bufs=6)
            dst = form[b, c, i][:]
            if i == 3:
                nc.vector.scalar_tensor_tensor(
                    out=dst, in0=cube[b, c, 3][:], scalar=0.0, in1=cube[b, c, 2][:], op0=ALU.max, op1=ALU.subtract
                )
            elif i == 7:
                nc.vector.scalar_tensor_tensor(
                    out=dst, in0=cube[b, c, 6][:], scalar=0.0, in1=cube[b, c, 7][:], op0=ALU.min, op1=ALU.subtract
                )
            else:
                source, j, k = (3, 3, 0) if i == 4 else (6, 2, 4)
                nc.vector.scalar_tensor_tensor(
                    out=dst, in0=cube[b, c, source][:], scalar=coef[k][:, c, j : j + 1],
                    in1=inner_term[b, c, i if i == 4 else 5][:], op0=ALU.mult, op1=ALU.add,
                )

        def inner_basis(b, c, j):
            if c == 0:
                inner[b, j] = planes.tile([P, CHUNKS, BLOCK], BF16, name="inner%d" % j, bufs=1)
            nc.vector.tensor_tensor(
                out=inner[b, j][:, c, :], in0=form[b, c, 3 if j == 2 else 4][:], in1=form[b, c, 6 if j == 2 else 7][:],
                op=ALU.min if j == 2 else ALU.max,
            )

        def regroup_inner(b, j, h):
            dst = new_group(b, h, PASS_2 if j == 2 else PASS_3)[:].rearrange("p (a i) t -> p a t i", i=4)
            src = inner[b, j][:, :, h * BANK : (h + 1) * BANK].rearrange("p t (a i) -> p a t i", i=4)
            nc.scalar.activation(out=dst, in_=src, func=ACT.Relu, scale=-1.0 if j == 2 else 1.0)

        def products(b, h, a):
            acc[b, h, a] = psum.tile([P, 2, UNITS], F32, name="acc", tag="acc")
            for t in range(2):
                cols = slice((2 * a + t) * P, (2 * a + t + 1) * P)
                for k in range(PASSES):
                    nc.tensor.matmul_mx(
                        out=acc[b, h, a][:, t, :],
                        lhsT=codes[b, h][:, k, cols].bitcast(FP8X4), lhsT_scale=scales[b, h][:, k, cols],
                        rhs=w_codes[:, k, :].bitcast(FP8X4), rhs_scale=w_scales[:, k, :],
                        start=(k == 0), stop=(k == PASSES - 1),
                    )

        def add_bias(b, h, a):
            result = rows_pool.tile([P, 2, UNITS], F32)
            nc.vector.tensor_add(out=result[:], in0=acc[b, h, a][:], in1=bias[:])
            nc.sync.dma_start(out=out_pairs[(b * BANKS + h) * 2 + a], in_=result[:])

        chunks = [(b, c) for b in range(BLOCKS) for c in range(CHUNKS)]
        steps = [chunk + (i,) for chunk in chunks for i in range(1, KNOTS - 1)]
        TERMS = {
            1: (0,), 2: (0, 1), 3: (0, 1), 4: (1, 4), 5: (4, 5), 6: (4, 5), 7: (4, 5), 8: (5,),
        }
        DONE = {4: 0, 5: 1, 7: 4, 8: 5}

        ALL_TILES = slice(0, TILES)

        def at(r, rank, job, args):
            jobs.setdefault((r, rank), []).append((job, args))

        for c in range(1, CHUNKS):
            at(3, 8, shifts_of, (c,))
        for k in range(PASSES):
            at(6 + 2 * k, 8, group_weights, (k,))
            at(6 + 2 * k + 1, 8, quantise_weights, (k,))
        for r, s in enumerate(steps):
            b, c, i = s
            at(r, 2, square_of, s)
            at(r + 2, 2, cube_of, s)
            for j in TERMS[i]:
                at(r + 3, 3, term_of, s + (j,))
            if i == 4 or i == 5:
                at(r + 3, 3, inner_term_of, s)
            if i in (3, 4, 6, 7):
                at(r + 4, 1, form_of, s)
            if i in (6, 7):
                at(r + 5, 1, inner_basis, (b, c, 2 if i == 6 else 3))
            if i in DONE:
                j = DONE[i]
                for h in range(BANKS):
                    n = r + (5, 6, 6, 7)[OUTER.index(j)] + h
                    at(n, 5, add_up, (b, c, j, h))
                    at(n + 2, 1, read_sum, (b, c, j, h))
                    if j == OUTER[-1]:
                        for a in range(2):
                            at(n + 2 + 1 + a, 6, transpose_back, (b, c, h, a))
                            at(n + 2 + 2 + a, 3, regroup, (b, c, h, a))
                        at(n + 7, 3, quantise, (b, h, 1 + c))
                        if c == CHUNKS - 1:
                            for a in range(2):
                                at(n + 8 + 2 * a, 7, products, (b, h, a))
                                at(n + 11 + 2 * a, 6, add_bias, (b, h, a))
            if c == CHUNKS - 1 and i in (6, 7):
                j = 2 if i == 6 else 3
                for h in range(BANKS):
                    at(r + 5 + 1 + h, 3, regroup_inner, (b, j, h))
                    at(r + 10 + h, 3, quantise, (b, h, PASS_2 if j == 2 else PASS_3))
            if c == 2 and i == 1:
                for h in range(BANKS):
                    at(r + 2 * h, 4, relu_branch, (b, h))
                    at(r + 2 * h + 3, 3, quantise, (b, h, 0))
            if i == 1 and c == 0 and b + 1 < BLOCKS:
                bank = b + 1
                at(r, 0, load_rows, (bank, ALL_TILES))
                at(r + 6, 3, row_statistics, (bank, ALL_TILES))
                for t in range(TILES):
                    at(r + 10 + t, 4, normalise, (bank, t))
                    at(r + 15 + 2 * t, 7, transpose_rows, (bank, t))
                    at(r + 15 + 2 * t + 1, 4, gamma_beta, (bank, t))

        one_tile = [slice(t, t + 1) for t in range(TILES)]
        for tiles in one_tile:
            load_rows(0, tiles)
        for tiles in one_tile:
            row_statistics(0, tiles)

        gamma = const.tile([P, CHUNKS], F32)
        beta = const.tile([P, CHUNKS], F32)
        bias = const.tile([P, 2, UNITS], F32)
        nc.vector.tensor_copy(out=gamma[:], in_=gamma_bf[:])
        nc.vector.tensor_copy(out=beta[:], in_=beta_bf[:])
        nc.vector.tensor_copy(out=bias[:, 0, :], in_=bias_bf[:])
        nc.vector.tensor_copy(out=bias[:, 1, :], in_=bias_bf[:])

        span = {}
        for s in (1, 2, 3, 4):
            span[s] = const.tile([P, CHUNKS, KNOTS - s], F32, name="span%d" % s)
            nc.vector.tensor_sub(out=span[s][:], in0=knots[:, :, s:KNOTS], in1=knots[:, :, 0 : KNOTS - s])

        weight = {}
        for k in range(5):
            others = [l for l in range(5) if l != k]
            prod = const.tile([P, CHUNKS, BASES], F32, name="prod%d" % k)
            gaps = [span[abs(k - l)][:, :, min(k, l) : min(k, l) + BASES] for l in others if abs(k - l) < 4]
            nc.vector.tensor_mul(out=prod[:], in0=gaps[0], in1=gaps[1])
            for gap in gaps[2:]:
                nc.vector.tensor_mul(out=prod[:], in0=prod[:], in1=gap)
            weight[k] = const.tile([P, CHUNKS, BASES], F32, name="weight%d" % k)
            nc.vector.reciprocal(out=weight[k][:], in_=prod[:])
            if 1 <= k <= 3:
                nc.vector.tensor_mul(out=weight[k][:], in0=weight[k][:], in1=span[4][:])
            if k % 2 == 1:
                nc.vector.tensor_scalar_mul(out=weight[k][:], in0=weight[k][:], scalar1=-1.0)

        FACTORS = {
            1: (1, 0, -1), 2: (0, 2, 1), 3: (1, 2, -1), 4: (4, 0, 1), 5: (4, 1, 1), 6: (3, 3, -1), 7: (4, 3, 1), 8: (3, 5, -1),
        }
        factor = const.tile([P, CHUNKS, KNOTS], F32)
        nc.vector.memset(factor[:], 1.0)
        for i in FACTORS:
            k, j, sign = FACTORS[i]
            nc.vector.tensor_scalar_mul(
                out=factor[:, :, i : i + 1], in0=weight[k][:, :, j : j + 1], scalar1=float(sign)
            )
        inv_factor = const.tile([P, CHUNKS, KNOTS], F32)
        nc.vector.reciprocal(out=inv_factor[:], in_=factor[:])
        root = const.tile([P, CHUNKS, KNOTS], F32)
        root_shift = const.tile([P, CHUNKS, KNOTS], F32)
        coef = {}
        for k in range(5):
            coef[k] = const.tile([P, CHUNKS, BASES], F32, name="coef%d" % k)
            nc.vector.tensor_mul(out=coef[k][:], in0=weight[k][:], in1=inv_factor[:, :, k : k + BASES])

        roots_of(0)
        shifts_of(0)
        w_raw = load_weights()
        for c in range(1, CHUNKS):
            roots_of(c)
        for t in range(TILES):
            normalise(0, t)
        for c in range(CHUNKS):
            transpose_rows(0, c)
            gamma_beta(0, c)
        for key in sorted(jobs):
            for job, args in jobs[key]:
                job(*args)
